import numpy as np
import ml_dtypes


def mxq(x, axis, fmt="e4m3"):
    dtype, down = {"e4m3": (ml_dtypes.float8_e4m3fn, 7), "e5m2": (ml_dtypes.float8_e5m2, 14)}[fmt]
    v = np.moveaxis(np.asarray(x, np.float32).astype(ml_dtypes.bfloat16).astype(np.float64), axis, -1)
    blocks = v.reshape(v.shape[:-1] + (-1, 32))
    amax = np.abs(blocks).max(-1, keepdims=True)
    byte = np.maximum(np.where(amax > 0, np.frexp(amax)[1] - 1 + 127, 0) - down, 1)
    scale = np.exp2(byte - 127.0)
    codes = (blocks / scale).astype(np.float32).astype(dtype).astype(np.float64)
    return np.moveaxis((codes * scale).reshape(v.shape), -1, axis)


WIDE = False


def mx_kscale(k):
    if not WIDE:
        return np.ones(k)
    levels = np.array([10, -10, 5, -5, 0])
    if k % 512:
        return np.exp2(np.random.permutation(np.resize(levels, k // 32))).repeat(32)
    a = np.empty((k // 512, 16))
    for p in range(k // 512):
        a[p, :8] = np.random.permutation(np.resize(levels, 8))
        for g in range(8):
            far = levels[np.abs(levels - a[p, g]) >= 10]
            a[p, g + 8] = far[np.random.randint(len(far))]
    return np.exp2(a.ravel()).repeat(32)


BF16 = ml_dtypes.bfloat16


def bf(x):
    return np.asarray(x, np.float32).astype(BF16)


def f64(x):
    return np.asarray(x).astype(np.float64)


E2M1 = np.array([0.0, 0.5, 1.0, 1.5, 2.0, 3.0, 4.0, 6.0, -0.0, -0.5, -1.0, -1.5, -2.0, -3.0, -4.0, -6.0])


def pack_weight(w, fmt):
    k, n = w.shape
    w = f64(bf(w)).reshape(k // 32, 32, n)
    amax = np.abs(w).max(1)
    if fmt == "e4m3":
        byte = np.frexp(amax)[1] - 1 + 127 - 7
    else:
        mant, ex = np.frexp(amax / 6.0)
        byte = np.where(mant > 0.5, ex, ex - 1) + 127
    byte = np.clip(np.where(amax > 0, byte, 1), 1, 254)
    scaled = (w * np.exp2(127.0 - byte)[:, None, :]).reshape(k, n).astype(np.float32)
    by_word = np.ascontiguousarray(scaled.reshape(k // 512, 128, 4, n).transpose(0, 1, 3, 2))
    if fmt == "e4m3":
        words = by_word.astype(ml_dtypes.float8_e4m3fn).view(np.uint8)
    else:
        c = by_word.astype(ml_dtypes.float4_e2m1fn).view(np.uint8) & 0xF
        words = c[..., 0::2] | (c[..., 1::2] << 4)
    return np.ascontiguousarray(words), np.ascontiguousarray(byte.astype(np.uint8).reshape(k // 512, 16, n))


def unpack_weight(words, scales, fmt):
    g, p, n, _ = words.shape
    if fmt == "e4m3":
        vals = np.ascontiguousarray(words).view(ml_dtypes.float8_e4m3fn).astype(np.float64)
    else:
        nib = np.empty((g, p, n, 4), np.uint8)
        nib[..., 0::2] = words & 0xF
        nib[..., 1::2] = words >> 4
        vals = E2M1[nib]
    vals = vals * np.repeat(np.exp2(scales.astype(np.float64) - 127.0), 8, axis=1)[..., None]
    return vals.transpose(0, 1, 3, 2).reshape(g * 512, n)
def pack4(w):
    words, scales = pack_weight(w, "e2m1")
    return words.reshape(words.shape[0], 128, -1), scales


def unpack4(words, scales):
    return unpack_weight(words.reshape(words.shape[0], 128, -1, 2), scales, "e2m1")


B, S, D, H = 16, 256, 512, 1024
HEAD = H // 2


def rotate_every_two(x):
    x1 = x[..., ::2]
    x2 = x[..., 1::2]
    return np.stack((-x2, x1), axis=-1).reshape(x.shape)


def rope_table(seq_len):
    pos = np.arange(seq_len, dtype=np.float64)
    inv = 10000.0 ** (np.arange(0, HEAD, 2, dtype=np.float64) / HEAD)
    radians = pos[:, None] / inv
    sincos = np.stack((np.sin(radians), np.cos(radians)), axis=-1).reshape(seq_len, -1)
    return np.repeat(sincos, 2, axis=-1)


def draw0():
    s = mx_kscale(D)
    u = np.repeat(mx_kscale(HEAD), 2)
    hidden_states = bf(np.random.standard_normal((B, S, D)) * s)
    Wq_words, Wq_scales = pack4((np.random.standard_normal((H, D)) / np.sqrt(D) / s * u[:, None]).T)
    bq = bf(np.random.standard_normal(H) * 0.3 * u)
    Wk_words, Wk_scales = pack4((np.random.standard_normal((H, D)) / np.sqrt(D) / s / u[:, None]).T)
    bk = bf(np.random.standard_normal(H) * 0.3 / u)
    return {"hidden_states": hidden_states,
            "Wq_words": Wq_words,
            "Wq_scales": Wq_scales,
            "bq": bq,
            "Wk_words": Wk_words,
            "Wk_scales": Wk_scales,
            "bk": bk}


def core(hidden_states, Wq_words, Wq_scales, bq, Wk_words, Wk_scales, bk):
    t = rope_table(hidden_states.shape[1])
    xq = mxq(f64(hidden_states), 2, "e4m3")
    q = (xq @ unpack4(Wq_words, Wq_scales)) + f64(bq)
    k = (xq @ unpack4(Wk_words, Wk_scales)) + f64(bk)
    q = q * t + rotate_every_two(q) * t
    k = k * t + rotate_every_two(k) * t
    return (mxq(q, 2, "e4m3") @ mxq(k, 2, "e4m3").transpose(0, 2, 1)) / np.sqrt(HEAD)


def e4m3fn_bytes(y):
    return np.clip(np.asarray(y, np.float64), -448.0, 448.0).astype(np.float32).astype(ml_dtypes.float8_e4m3fn).view(np.uint8)


def e4m3fn_values(b):
    return np.asarray(b, np.uint8).view(ml_dtypes.float8_e4m3fn).astype(np.float64)


def setup_inputs():
    d = draw0()
    x0 = np.asarray(d['hidden_states']).astype(np.float64)
    s = (np.max(np.abs(x0), axis=(0, 1), keepdims=True) / 448.0).astype(np.float32)
    out = {}
    for k, v in d.items():
        if k == 'hidden_states':
            out['hidden_states_bytes'] = e4m3fn_bytes(x0 / s.astype(np.float64))
            out['hidden_states_scale'] = s
        else:
            out[k] = v
    return out


def reference(hidden_states_bytes, hidden_states_scale, Wq_words, Wq_scales, bq, Wk_words, Wk_scales, bk):
    return core(e4m3fn_values(hidden_states_bytes) * hidden_states_scale.astype(np.float64), Wq_words, Wq_scales, bq, Wk_words, Wk_scales, bk)

@@ -1,0 +1,350 @@
+import math
+from contextlib import ExitStack
+
+import concourse.mybir as mybir
+from concourse.masks import make_identity
+
+F32 = mybir.dt.float32
+BF16 = mybir.dt.bfloat16
+I32 = mybir.dt.int32
+U32 = mybir.dt.uint32
+U8 = mybir.dt.uint8
+FP8 = mybir.dt.float8_e4m3fn
+FP8X4 = mybir.dt.float8_e4m3fn_x4
+FP4X4 = mybir.dt.float4_e2m1fn_x4
+ALU = mybir.AluOpType
+ACT = mybir.ActivationFunctionType
+
+P = 128
+B, S, D, H = 16, 256, 512, 1024
+HEAD = H // 2
+TOK = 512
+GROUPS = B * S // TOK
+NT = TOK // P
+PASSES = H // 512
+BLOCKS = [(0, 0), (0, 1), (1, 0), (1, 1)]
+NB = 4 * GROUPS
+
+FLOPS = 2 * B * S * D * 2 * H + 2 * B * S * S * H
+
+
+def tile_ropeattention_pa_t_w4_kernel(
+    tc, hidden_bytes, hidden_scale, wq_words, wq_scales, bq, wk_words, wk_scales, bk, out
+):
+    nc = tc.nc
+    with ExitStack() as ctx:
+        keep = ctx.enter_context(tc.tile_pool(name="keep", bufs=1))
+        xin = ctx.enter_context(tc.tile_pool(name="xin", bufs=GROUPS))
+        work = ctx.enter_context(tc.tile_pool(name="work", bufs=2))
+        roll = ctx.enter_context(tc.tile_pool(name="roll", bufs=4))
+        ps_qk = ctx.enter_context(tc.psum_pool(name="ps_qk", bufs=5))
+        ps_aux = ctx.enter_context(tc.psum_pool(name="ps_aux", bufs=3))
+        ctx.enter_context(tc.manual_schedule())
+
+        tokens = hidden_bytes.rearrange("b s k -> (b s) k")
+
+        scale_bc = keep.tile([P, D], F32)
+        nc.scalar.dma_start(out=scale_bc[:], in_=hidden_scale.rearrange("a b k -> (a b k)").partition_broadcast(P))
+
+        x_bytes = []
+        for grp in range(GROUPS):
+            xb = xin.tile([P, NT, D], U8, name="xb", align_bytes=64)
+            x_bytes.append(xb)
+
+        def load_x(grp, n0, n1):
+            rows = tokens[grp * TOK : (grp + 1) * TOK, :].rearrange("(n p) k -> p n k", p=P)
+            nc.sync.dma_start(out=x_bytes[grp][:, n0:n1, :], in_=rows[:, n0:n1, :])
+
+        load_x(0, 0, 2)
+        load_x(0, 2, 4)
+        wraw = keep.tile([P, 2, 2 * H], U8, align_bytes=64)
+        sraw = keep.tile([P, 2, H], U8, align_bytes=64)
+        nc.sync.dma_start(out=wraw[:, 0, :], in_=wq_words[0])
+
+        p_int = keep.tile([P, 1], I32)
+        nc.gpsimd.iota(p_int[:], pattern=[[0, 1]], base=0, channel_multiplier=1)
+        s_f = keep.tile([P, S], F32)
+        nc.gpsimd.iota(s_f[:], pattern=[[1, S]], base=0, channel_multiplier=0, allow_small_or_imprecise_dtypes=True)
+        nc.gpsimd.memset(sraw[:].rearrange("p a n -> p (a n)").bitcast(I32), 0)
+        ident = keep.tile([P, P], F32)
+        make_identity(nc, ident[:])
+
+        for i, s in enumerate((wq_scales, wk_scales)):
+            for q in range(4):
+                nc.sync.dma_start(
+                    out=sraw[32 * q : 32 * q + 4, i, :].bitcast(I32),
+                    in_=s[0, 4 * q : 4 * q + 4, :].bitcast(I32),
+                )
+        braw = []
+        for i, b in enumerate((bq, bk)):
+            br = keep.tile([P, PASSES, 4], BF16, name="br%d" % i)
+            nc.sync.dma_start(out=br[:], in_=b.rearrange("(g p r) -> p g r", p=P, r=4))
+            braw.append(br)
+        nc.sync.dma_start(out=wraw[:, 1, :], in_=wk_words[0])
+        for grp in range(1, GROUPS):
+            load_x(grp, 0, NT)
+
+        rho = 10000.0 ** (-1.0 / (HEAD // 2))
+        bits = keep.tile([P, 7], I32)
+        fac = keep.tile([P, 7], F32)
+        for b in range(7):
+            nc.vector.tensor_single_scalar(out=bits[:, b : b + 1], in_=p_int[:], scalar=1 << b, op=ALU.bitwise_and)
+        for b in range(7):
+            nc.vector.tensor_scalar(
+                out=fac[:, b : b + 1], in0=bits[:, b : b + 1],
+                scalar1=(rho ** (1 << b) - 1.0) / (1 << b), scalar2=1.0, op0=ALU.mult, op1=ALU.add,
+            )
+        f3 = keep.tile([P, 3], F32)
+        nc.vector.tensor_tensor(out=f3[:], in0=fac[:, 0:3], in1=fac[:, 3:6], op=ALU.mult)
+        f1 = keep.tile([P, 3], F32)
+        nc.vector.tensor_tensor(out=f1[:, 0:1], in0=f3[:, 0:1], in1=fac[:, 6:7], op=ALU.mult)
+        nc.vector.tensor_tensor(out=f1[:, 1:2], in0=f3[:, 1:2], in1=f3[:, 2:3], op=ALU.mult)
+        omega = keep.tile([P, PASSES], F32)
+        nc.vector.tensor_tensor(out=omega[:, 0:1], in0=f1[:, 0:1], in1=f1[:, 1:2], op=ALU.mult)
+        nc.vector.tensor_scalar(
+            out=omega[:, 1:2], in0=omega[:, 0:1], scalar1=rho**P, scalar2=None, op0=ALU.mult
+        )
+        ang = keep.tile([P, 4, S], F32)
+        turns = keep.tile([P, 4, S], I32)
+        red1 = keep.tile([P, 4, S], F32)
+        red2 = keep.tile([P, 4, S], F32)
+        table = keep.tile([P, 4, TOK], F32)
+        c1 = 6.28125
+
+        def make_table(g):
+            two = slice(2 * g, 2 * g + 2)
+            nc.vector.tensor_scalar(
+                out=ang[:, 2 * g, :], in0=s_f[:], scalar1=omega[:, g : g + 1], scalar2=None, op0=ALU.mult
+            )
+            nc.vector.tensor_scalar(
+                out=ang[:, 2 * g + 1, :], in0=s_f[:], scalar1=omega[:, g : g + 1], scalar2=math.pi / 2.0,
+                op0=ALU.mult, op1=ALU.add,
+            )
+            nc.vector.tensor_scalar(
+                out=turns[:, two], in0=ang[:, two], scalar1=1.0 / (2.0 * math.pi), scalar2=None, op0=ALU.mult
+            )
+            nc.vector.scalar_tensor_tensor(
+                out=red1[:, two], in0=turns[:, two], scalar=-c1, in1=ang[:, two], op0=ALU.mult, op1=ALU.add
+            )
+            nc.vector.scalar_tensor_tensor(
+                out=red2[:, two], in0=turns[:, two], scalar=c1 - 2.0 * math.pi, in1=red1[:, two],
+                op0=ALU.mult, op1=ALU.add,
+            )
+            for rep in range(TOK // S):
+                nc.scalar.activation(out=table[:, two, rep * S : (rep + 1) * S], in_=red2[:, two], func=ACT.Sin)
+
+        wperm = keep.tile([P, 2, PASSES, 4, 2 * P], U8, align_bytes=64)
+        sperm = keep.tile([P, 2, PASSES, 4, P], U8, align_bytes=64)
+
+        def permute_words(i, g):
+            nc.vector.tensor_copy(
+                out=wperm[:, i, g].rearrange("p r (c b) -> p r c b", b=2),
+                in_=wraw[:, i, g * 1024 : (g + 1) * 1024].rearrange("p (c r b) -> p r c b", r=4, b=2),
+            )
+
+        def permute_scales(i, g):
+            nc.vector.tensor_copy(
+                out=sperm[:, i, g], in_=sraw[:, i, g * 512 : (g + 1) * 512].rearrange("p (c r) -> p r c", r=4)
+            )
+
+        x_wide = {}
+        x_tr = {}
+        x_grp = {}
+        x_neg = {}
+        x_q = {}
+        qk_q = {}
+        planes = {}
+        inter = {}
+        lifted = {}
+        banks = {}
+
+        def widen(grp, n):
+            if n == 0:
+                xw = work.tile([P, NT, D], BF16, name="xw", align_bytes=64)
+                x_wide[grp] = xw
+            nc.vector.tensor_tensor(
+                out=x_wide[grp][:, n, :], in0=x_bytes[grp][:, n, :].bitcast(FP8), in1=scale_bc[:], op=ALU.mult
+            )
+
+        def turn(grp, half):
+            bank = ps_aux.tile([P, 2, 2, P], F32, name="bank_tr", tag="aux")
+            x_tr[grp, half] = bank
+            for n in range(2):
+                words = x_wide[grp][:, 2 * half + n, :].bitcast(F32)
+                for u in range(2):
+                    nc.tensor.transpose(bank[:, n, u, :], words[:, u : D // 2 : 2], ident[:])
+
+        def leave(grp, half):
+            if half == 0:
+                xg = work.tile([P, TOK, 4], BF16, name="xg", align_bytes=64)
+                x_grp[grp] = xg
+            words = x_grp[grp][:].rearrange("p t j -> p (t j)").bitcast(F32)
+            nc.scalar.copy(
+                out=words[:, half * 512 : (half + 1) * 512].rearrange("p (n r u) -> p n r u", n=2, u=2),
+                in_=x_tr[grp, half][:].rearrange("p n u r -> p n r u"),
+            )
+
+        def negate(grp):
+            xn = work.tile([P, TOK, 4], BF16, name="xn", align_bytes=64)
+            x_neg[grp] = xn
+            nc.vector.tensor_scalar(out=xn[:], in0=x_grp[grp][:], scalar1=-1.0, scalar2=None, op0=ALU.mult)
+
+        def quant_x(grp, sign):
+            codes = work.tile([P, TOK], U32, name="xc%d" % sign, align_bytes=64)
+            scales = work.tile([P, TOK], U8, name="xs%d" % sign, align_bytes=64)
+            x_q[grp, sign] = (codes, scales)
+            src = (x_grp if sign == 0 else x_neg)[grp]
+            nc.vector.quantize_mx(
+                out=codes[:].bitcast(FP8X4), scales=scales[:], in_=src[:].rearrange("p t j -> p (t j)")
+            )
+
+        bias = keep.tile([P, 2, PASSES, 4], F32)
+
+        def make_bias(i):
+            raw = braw[i][:].rearrange("p g (h two) -> p (g h) two", two=2)
+            res = bias[:, i].rearrange("p g (h two) -> p (g h) two", two=2)
+            nc.vector.tensor_tensor(out=res[:, :, 0], in0=raw[:, :, 0], in1=raw[:, :, 1], op=ALU.subtract)
+            nc.vector.tensor_tensor(out=res[:, :, 1], in0=raw[:, :, 0], in1=raw[:, :, 1], op=ALU.add)
+
+        def project(blk, r):
+            grp, j = divmod(blk, 4)
+            i, g = BLOCKS[j]
+            acc = ps_qk.tile([P, TOK], F32, name="acc")
+            banks[blk, r] = acc
+            first = r // 2 * 2
+            for half in range(2):
+                sign = 1 if (half == 1 and r % 2 == 0) else 0
+                codes, scales = x_q[grp, sign]
+                nc.tensor.matmul_mx(
+                    out=acc[:],
+                    lhsT=wperm[:, i, g, first + half, :].bitcast(FP4X4),
+                    lhsT_scale=sperm[:, i, g, first + half, :],
+                    rhs=codes[:].bitcast(FP8X4),
+                    rhs_scale=scales[:],
+                    start=(half == 0),
+                    stop=(half == 1),
+                )
+
+        def new_planes(blk):
+            pl = roll.tile([P, 4, TOK], BF16, name="pl", align_bytes=64)
+            planes[blk] = pl
+
+        def rotate(blk, r):
+            i, g = BLOCKS[blk % 4]
+            nc.vector.scalar_tensor_tensor(
+                out=planes[blk][:, r, :], in0=banks[blk, r][:], scalar=bias[:, i, g, r : r + 1],
+                in1=table[:, 2 * g + r // 2, :], op0=ALU.add, op1=ALU.mult,
+            )
+
+        def lift(blk, r):
+            i, g = BLOCKS[blk % 4]
+            z = roll.tile([P, TOK], F32, name="z")
+            lifted[blk] = z
+            nc.scalar.activation(
+                out=z[:], in_=banks[blk, r][:], func=ACT.Identity, bias=bias[:, i, g, r : r + 1], scale=1.0
+            )
+
+        def mark(blk, r):
+            nc.vector.memset(planes[blk][:, r, 0:16], 0.0)
+
+        def rotate_gp(blk, r):
+            i, g = BLOCKS[blk % 4]
+            nc.gpsimd.tensor_tensor(
+                out=planes[blk][:, r, :], in0=lifted[blk][:], in1=table[:, 2 * g + r // 2, :], op=ALU.mult
+            )
+
+        def interleave(blk, c0, c1, eng):
+            if c0 == 0:
+                qi = roll.tile([P, TOK, 4], BF16, name="qi", align_bytes=64)
+                inter[blk] = qi
+            eng(
+                out=inter[blk][:, c0:c1, :].rearrange("p (c i) t -> p c t i", i=4),
+                in_=planes[blk][:, :, c0:c1].rearrange("p t (c i) -> p c t i", i=4),
+            )
+
+        def quant_qk(blk, c0, c1):
+            j = blk % 4
+            if c0 == 0:
+                codes = roll.tile([P, TOK], U32, name="qc%d" % j, align_bytes=64)
+                scales = roll.tile([P, TOK], U8, name="qs%d" % j, align_bytes=64)
+                qk_q[blk] = (codes, scales)
+            codes, scales = qk_q[blk]
+            nc.vector.quantize_mx(
+                out=codes[:, c0:c1].bitcast(FP8X4), scales=scales[:, c0:c1],
+                in_=inter[blk][:, c0:c1, :].rearrange("p t j -> p (t j)"),
+            )
+
+        def scores(grp, b):
+            sc = ps_aux.tile([P, 2, S], F32, name="sc", tag="aux")
+            for m in range(2):
+                for g in range(PASSES):
+                    qcod, qsc = qk_q[4 * grp + g]
+                    kcod, ksc = qk_q[4 * grp + PASSES + g]
+                    rows = slice(b * S + m * P, b * S + (m + 1) * P)
+                    cols = slice(b * S, (b + 1) * S)
+                    nc.tensor.matmul_mx(
+                        out=sc[:, m, :],
+                        lhsT=qcod[:, rows].bitcast(FP8X4), lhsT_scale=qsc[:, rows],
+                        rhs=kcod[:, cols].bitcast(FP8X4), rhs_scale=ksc[:, cols],
+                        start=(g == 0), stop=(g == PASSES - 1),
+                    )
+            res = roll.tile([P, 2, S], F32, name="res")
+            nc.scalar.activation(out=res[:], in_=sc[:], func=ACT.Copy, scale=1.0 / math.sqrt(HEAD))
+            nc.sync.dma_start(out=out[grp * 2 + b].rearrange("(m p) n -> p m n", p=P), in_=res[:])
+
+        make_table(0)
+        for half in range(2):
+            widen(0, 2 * half)
+            widen(0, 2 * half + 1)
+            turn(0, half)
+            leave(0, half)
+        permute_words(0, 0)
+        quant_x(0, 0)
+        permute_scales(0, 0)
+        negate(0)
+        quant_x(0, 1)
+        make_bias(0)
+
+        for blk in range(NB):
+            grp, j = divmod(blk, 4)
+            new_planes(blk)
+            for r in (1, 0, 3, 2):
+                project(blk, r)
+                rotate(blk, r)
+            if grp + 1 < GROUPS and j == 1:
+                for half in range(2):
+                    turn(grp + 1, half)
+                    leave(grp + 1, half)
+            if blk < NB - 1:
+                interleave(blk, 0, TOK, nc.scalar.copy)
+            if blk == 0:
+                make_table(1)
+                permute_words(0, 1)
+                permute_scales(0, 1)
+                make_bias(1)
+            if blk == 1:
+                permute_words(1, 0)
+                permute_scales(1, 0)
+            if blk == 2:
+                permute_words(1, 1)
+                permute_scales(1, 1)
+            if blk > 0:
+                quant_qk(blk - 1, 0, TOK)
+            if grp + 1 < GROUPS:
+                if j == 0:
+                    for n in range(NT):
+                        widen(grp + 1, n)
+                if j == 2:
+                    quant_x(grp + 1, 0)
+                    negate(grp + 1)
+                    quant_x(grp + 1, 1)
+            if grp > 0 and j == 1:
+                scores(grp - 1, 0)
+            if grp > 0 and j == 2:
+                scores(grp - 1, 1)
+
+        interleave(NB - 1, 0, S, nc.vector.tensor_copy)
+        interleave(NB - 1, S, TOK, nc.scalar.copy)
+        for b in range(2):
+            quant_qk(NB - 1, b * S, (b + 1) * S)
+            scores(GROUPS - 1, b)

@@ -24,7 +24,9 @@ NT = TOK // P
 PASSES = H // 512
 BLOCKS = [(0, 0), (0, 1), (1, 0), (1, 1)]
 NB = 4 * GROUPS
+SCALAR_GROUPS = [1,2,3,4,5,6,7]
 
+S_COLS = 256
 FLOPS = 2 * B * S * D * 2 * H + 2 * B * S * S * H
 
 
@@ -35,7 +37,7 @@ def tile_ropeattention_pa_t_w4_kernel(
     with ExitStack() as ctx:
         keep = ctx.enter_context(tc.tile_pool(name="keep", bufs=1))
         xin = ctx.enter_context(tc.tile_pool(name="xin", bufs=GROUPS))
-        work = ctx.enter_context(tc.tile_pool(name="work", bufs=2))
+        work = ctx.enter_context(tc.tile_pool(name="work", bufs=3))
         roll = ctx.enter_context(tc.tile_pool(name="roll", bufs=4))
         ps_qk = ctx.enter_context(tc.psum_pool(name="ps_qk", bufs=5))
         ps_aux = ctx.enter_context(tc.psum_pool(name="ps_aux", bufs=3))
@@ -45,6 +47,9 @@ def tile_ropeattention_pa_t_w4_kernel(
 
         scale_bc = keep.tile([P, D], F32)
         nc.scalar.dma_start(out=scale_bc[:], in_=hidden_scale.rearrange("a b k -> (a b k)").partition_broadcast(P))
+
+        scale_col = keep.tile([P, 4], F32)
+        nc.scalar.dma_start(out=scale_col[:], in_=hidden_scale.rearrange("a b (p t) -> p (a b t)", t=4))
 
         x_bytes = []
         for grp in range(GROUPS):
@@ -60,6 +65,7 @@ def tile_ropeattention_pa_t_w4_kernel(
         wraw = keep.tile([P, 2, 2 * H], U8, align_bytes=64)
         sraw = keep.tile([P, 2, H], U8, align_bytes=64)
         nc.sync.dma_start(out=wraw[:, 0, :], in_=wq_words[0])
+        load_x(1, 0, NT)
 
         p_int = keep.tile([P, 1], I32)
         nc.gpsimd.iota(p_int[:], pattern=[[0, 1]], base=0, channel_multiplier=1)
@@ -81,7 +87,7 @@ def tile_ropeattention_pa_t_w4_kernel(
             nc.sync.dma_start(out=br[:], in_=b.rearrange("(g p r) -> p g r", p=P, r=4))
             braw.append(br)
         nc.sync.dma_start(out=wraw[:, 1, :], in_=wk_words[0])
-        for grp in range(1, GROUPS):
+        for grp in range(2, GROUPS):
             load_x(grp, 0, NT)
 
         rho = 10000.0 ** (-1.0 / (HEAD // 2))
@@ -89,6 +95,10 @@ def tile_ropeattention_pa_t_w4_kernel(
         fac = keep.tile([P, 7], F32)
         for b in range(7):
             nc.vector.tensor_single_scalar(out=bits[:, b : b + 1], in_=p_int[:], scalar=1 << b, op=ALU.bitwise_and)
+        half_pi = keep.tile([P, 1], F32)
+        nc.vector.tensor_scalar(
+            out=half_pi[:], in0=p_int[:], scalar1=0.0, scalar2=math.pi / 2.0, op0=ALU.mult, op1=ALU.add
+        )
         for b in range(7):
             nc.vector.tensor_scalar(
                 out=fac[:, b : b + 1], in0=bits[:, b : b + 1],
@@ -96,42 +106,46 @@ def tile_ropeattention_pa_t_w4_kernel(
             )
         f3 = keep.tile([P, 3], F32)
         nc.vector.tensor_tensor(out=f3[:], in0=fac[:, 0:3], in1=fac[:, 3:6], op=ALU.mult)
-        f1 = keep.tile([P, 3], F32)
-        nc.vector.tensor_tensor(out=f1[:, 0:1], in0=f3[:, 0:1], in1=fac[:, 6:7], op=ALU.mult)
-        nc.vector.tensor_tensor(out=f1[:, 1:2], in0=f3[:, 1:2], in1=f3[:, 2:3], op=ALU.mult)
-        omega = keep.tile([P, PASSES], F32)
-        nc.vector.tensor_tensor(out=omega[:, 0:1], in0=f1[:, 0:1], in1=f1[:, 1:2], op=ALU.mult)
+        f2 = keep.tile([P, 2], F32)
+        nc.vector.tensor_tensor(out=f2[:, 0:1], in0=f3[:, 0:1], in1=fac[:, 6:7], op=ALU.mult)
+        nc.vector.tensor_tensor(out=f2[:, 1:2], in0=f3[:, 1:2], in1=f3[:, 2:3], op=ALU.mult)
+        omega = keep.tile([P, 3], F32)
+        nc.vector.tensor_tensor(out=omega[:, 0:1], in0=f2[:, 0:1], in1=f2[:, 1:2], op=ALU.mult)
         nc.vector.tensor_scalar(
             out=omega[:, 1:2], in0=omega[:, 0:1], scalar1=rho**P, scalar2=None, op0=ALU.mult
         )
-        ang = keep.tile([P, 4, S], F32)
-        turns = keep.tile([P, 4, S], I32)
-        red1 = keep.tile([P, 4, S], F32)
-        red2 = keep.tile([P, 4, S], F32)
+        nc.vector.tensor_scalar(
+            out=omega[:, 2:3], in0=omega[:, 1:2], scalar1=-1.0, scalar2=None, op0=ALU.mult
+        )
+        ang = keep.tile([P, S], F32)
+        turns = keep.tile([P, S], I32)
+        red1 = keep.tile([P, S], F32)
+        red2 = keep.tile([P, S], F32)
+        red3 = keep.tile([P, S], F32)
         table = keep.tile([P, 4, TOK], F32)
         c1 = 6.28125
+        nc.vector.tensor_scalar(out=ang[:], in0=s_f[:], scalar1=omega[:, 0:1], scalar2=None, op0=ALU.mult)
+        nc.vector.tensor_scalar(
+            out=turns[:], in0=ang[:], scalar1=1.0 / (2.0 * math.pi), scalar2=None, op0=ALU.mult
+        )
+        nc.vector.scalar_tensor_tensor(out=red1[:], in0=turns[:], scalar=-c1, in1=ang[:], op0=ALU.mult, op1=ALU.add)
+        nc.vector.scalar_tensor_tensor(
+            out=red2[:], in0=turns[:], scalar=c1 - 2.0 * math.pi, in1=red1[:], op0=ALU.mult, op1=ALU.add
+        )
 
         def make_table(g):
-            two = slice(2 * g, 2 * g + 2)
-            nc.vector.tensor_scalar(
-                out=ang[:, 2 * g, :], in0=s_f[:], scalar1=omega[:, g : g + 1], scalar2=None, op0=ALU.mult
-            )
-            nc.vector.tensor_scalar(
-                out=ang[:, 2 * g + 1, :], in0=s_f[:], scalar1=omega[:, g : g + 1], scalar2=math.pi / 2.0,
-                op0=ALU.mult, op1=ALU.add,
-            )
-            nc.vector.tensor_scalar(
-                out=turns[:, two], in0=ang[:, two], scalar1=1.0 / (2.0 * math.pi), scalar2=None, op0=ALU.mult
-            )
-            nc.vector.scalar_tensor_tensor(
-                out=red1[:, two], in0=turns[:, two], scalar=-c1, in1=ang[:, two], op0=ALU.mult, op1=ALU.add
-            )
-            nc.vector.scalar_tensor_tensor(
-                out=red2[:, two], in0=turns[:, two], scalar=c1 - 2.0 * math.pi, in1=red1[:, two],
-                op0=ALU.mult, op1=ALU.add,
-            )
+            if g == 0:
+                nc.scalar.activation(out=red3[:], in_=red2[:], func=ACT.Abs)
             for rep in range(TOK // S):
-                nc.scalar.activation(out=table[:, two, rep * S : (rep + 1) * S], in_=red2[:, two], func=ACT.Sin)
+                cols = slice(rep * S, (rep + 1) * S)
+                if g == 0:
+                    nc.scalar.activation(out=table[:, 0, cols], in_=red2[:], func=ACT.Sin)
+                    nc.scalar.activation(out=table[:, 1, cols], in_=red3[:], func=ACT.Sin, bias=half_pi[:], scale=-1.0)
+                else:
+                    nc.scalar.activation(out=table[:, 2, cols], in_=s_f[:], func=ACT.Sin, scale=omega[:, 1:2])
+                    nc.scalar.activation(
+                        out=table[:, 3, cols], in_=s_f[:], func=ACT.Sin, bias=half_pi[:], scale=omega[:, 2:3]
+                    )
 
         wperm = keep.tile([P, 2, PASSES, 4, 2 * P], U8, align_bytes=64)
         sperm = keep.tile([P, 2, PASSES, 4, P], U8, align_bytes=64)
@@ -151,6 +165,8 @@ def tile_ropeattention_pa_t_w4_kernel(
         x_tr = {}
         x_grp = {}
         x_neg = {}
+        x_pl = {}
+        sc_bank = {}
         x_q = {}
         qk_q = {}
         planes = {}
@@ -166,6 +182,15 @@ def tile_ropeattention_pa_t_w4_kernel(
                 out=x_wide[grp][:, n, :], in0=x_bytes[grp][:, n, :].bitcast(FP8), in1=scale_bc[:], op=ALU.mult
             )
 
+        def widen_plain(grp, n0, n1):
+            if n0 == 0:
+                xw = work.tile([P, NT, D], BF16, name="xw", align_bytes=64)
+                x_wide[grp] = xw
+            nc.scalar.copy(
+                out=x_wide[grp][:, n0:n1, :].rearrange("p n k -> p (n k)"),
+                in_=x_bytes[grp][:, n0:n1, :].rearrange("p n k -> p (n k)").bitcast(FP8),
+            )
+
         def turn(grp, half):
             bank = ps_aux.tile([P, 2, 2, P], F32, name="bank_tr", tag="aux")
             x_tr[grp, half] = bank
@@ -174,14 +199,42 @@ def tile_ropeattention_pa_t_w4_kernel(
                 for u in range(2):
                     nc.tensor.transpose(bank[:, n, u, :], words[:, u : D // 2 : 2], ident[:])
 
+        def turn_plain(grp, u):
+            bank = ps_aux.tile([P, NT, P], F32, name="bank_tu", tag="aux")
+            x_tr[grp, u] = bank
+            for n in range(NT):
+                words = x_wide[grp][:, n, :].bitcast(F32)
+                nc.tensor.transpose(bank[:, n, :], words[:, u : D // 2 : 2], ident[:])
+
+        def new_xg(grp):
+            xg = work.tile([P, TOK, 4], BF16, name="xg", align_bytes=64)
+            x_grp[grp] = xg
+
         def leave(grp, half):
             if half == 0:
-                xg = work.tile([P, TOK, 4], BF16, name="xg", align_bytes=64)
-                x_grp[grp] = xg
+                new_xg(grp)
             words = x_grp[grp][:].rearrange("p t j -> p (t j)").bitcast(F32)
             nc.scalar.copy(
                 out=words[:, half * 512 : (half + 1) * 512].rearrange("p (n r u) -> p n r u", n=2, u=2),
                 in_=x_tr[grp, half][:].rearrange("p n u r -> p n r u"),
+            )
+
+        def leave_scaled(grp, t):
+            if t == 0:
+                xp = work.tile([P, 4, TOK], BF16, name="xp", align_bytes=64)
+                x_pl[grp] = xp
+            u, e = divmod(t, 2)
+            pairs = x_tr[grp, u][:].rearrange("p n r -> p (n r)").bitcast(BF16).rearrange("p (c e) -> p c e", e=2)
+            nc.scalar.activation(
+                out=x_pl[grp][:, t, :], in_=pairs[:, :, e], func=ACT.Copy, scale=scale_col[:, t : t + 1]
+            )
+
+        def zip_x(grp, c0, c1):
+            if c0 == 0:
+                new_xg(grp)
+            nc.scalar.copy(
+                out=x_grp[grp][:, c0:c1, :].rearrange("p (c i) t -> p c t i", i=4),
+                in_=x_pl[grp][:, :, c0:c1].rearrange("p t (c i) -> p c t i", i=4),
             )
 
         def negate(grp):
@@ -236,23 +289,6 @@ def tile_ropeattention_pa_t_w4_kernel(
                 in1=table[:, 2 * g + r // 2, :], op0=ALU.add, op1=ALU.mult,
             )
 
-        def lift(blk, r):
-            i, g = BLOCKS[blk % 4]
-            z = roll.tile([P, TOK], F32, name="z")
-            lifted[blk] = z
-            nc.scalar.activation(
-                out=z[:], in_=banks[blk, r][:], func=ACT.Identity, bias=bias[:, i, g, r : r + 1], scale=1.0
-            )
-
-        def mark(blk, r):
-            nc.vector.memset(planes[blk][:, r, 0:16], 0.0)
-
-        def rotate_gp(blk, r):
-            i, g = BLOCKS[blk % 4]
-            nc.gpsimd.tensor_tensor(
-                out=planes[blk][:, r, :], in0=lifted[blk][:], in1=table[:, 2 * g + r // 2, :], op=ALU.mult
-            )
-
         def interleave(blk, c0, c1, eng):
             if c0 == 0:
                 qi = roll.tile([P, TOK, 4], BF16, name="qi", align_bytes=64)
@@ -260,6 +296,12 @@ def tile_ropeattention_pa_t_w4_kernel(
             eng(
                 out=inter[blk][:, c0:c1, :].rearrange("p (c i) t -> p c t i", i=4),
                 in_=planes[blk][:, :, c0:c1].rearrange("p t (c i) -> p c t i", i=4),
+            )
+
+        def zip_gp(blk, c0, c1):
+            nc.gpsimd.tensor_scalar(
+                out=inter[blk][:, c0:c1, :], in0=planes[blk][:, :, c0:c1].rearrange("p t c -> p c t"),
+                scalar1=1.0, scalar2=1.0, op0=ALU.mult, op1=ALU.mult,
             )
 
         def quant_qk(blk, c0, c1):
@@ -276,6 +318,7 @@ def tile_ropeattention_pa_t_w4_kernel(
 
         def scores(grp, b):
             sc = ps_aux.tile([P, 2, S], F32, name="sc", tag="aux")
+            sc_bank[grp, b] = sc
             for m in range(2):
                 for g in range(PASSES):
                     qcod, qsc = qk_q[4 * grp + g]
@@ -288,37 +331,97 @@ def tile_ropeattention_pa_t_w4_kernel(
                         rhs=kcod[:, cols].bitcast(FP8X4), rhs_scale=ksc[:, cols],
                         start=(g == 0), stop=(g == PASSES - 1),
                     )
+
+        def store(grp, b):
             res = roll.tile([P, 2, S], F32, name="res")
-            nc.scalar.activation(out=res[:], in_=sc[:], func=ACT.Copy, scale=1.0 / math.sqrt(HEAD))
+            nc.scalar.activation(out=res[:], in_=sc_bank[grp, b][:], func=ACT.Copy, scale=1.0 / math.sqrt(HEAD))
             nc.sync.dma_start(out=out[grp * 2 + b].rearrange("(m p) n -> p m n", p=P), in_=res[:])
 
-        make_table(0)
+        XI = dict(wp0=-9, wp1=-8, t=-7, l0=-6, l1=-6, l2=-5, l3=-5, z0=-4, z1=-3, neg=-2, q0=-2, q1=-2)
+        X4 = dict(w0=-8, w1=-8, w2=-7, w3=-6, t0=-6, t1=-5, l0=-5, l1=-4, neg=-3, q0=-3, q1=-2)
+        XI1 = dict(wp0=-1, wp1=-1, t=0, l0=0, l1=0, l2=1, l3=1, z0=2, z1=2, neg=2, q0=2, q1=2)
+        X41 = dict(w0=-1, w1=-1, w2=0, w3=0, t0=0, t1=1, l0=1, l1=1, neg=2, q0=2, q1=2)
+
+        def steps(slot, which):
+            for grp in range(1, GROUPS):
+                scal = grp in SCALAR_GROUPS
+                plan = (XI1 if scal else X41) if grp == 1 else (XI if scal else X4)
+                shift = 0 if grp == 1 else 4 * grp
+                for key in plan:
+                    if max(plan[key] + shift, -1) == slot:
+                        which(grp, scal, key)
+
+        def scalar_step(grp, scal, key):
+            if key in ("wp0", "wp1"):
+                n = 2 * int(key[2])
+                widen_plain(grp, n, n + 2)
+            elif key[0] == "l":
+                (leave_scaled if scal else leave)(grp, int(key[1]))
+            elif key[0] == "z":
+                zip_x(grp, S * int(key[1]), S * (int(key[1]) + 1))
+
+        def tensor_step(grp, scal, key):
+            if key == "t":
+                turn_plain(grp, 0)
+                turn_plain(grp, 1)
+            elif key[0] == "t":
+                turn(grp, int(key[1]))
+
+        def vector_step(grp, scal, key):
+            if key[0] == "w" and not scal:
+                widen(grp, int(key[1]))
+            elif key == "neg":
+                negate(grp)
+            elif key[0] == "q":
+                quant_x(grp, int(key[1]))
+
+        def scalar_x(slot):
+            steps(slot, scalar_step)
+
+        def tensor_x(slot):
+            steps(slot, tensor_step)
+
+        def vector_x(slot):
+            steps(slot, vector_step)
+
+        def early(slot):
+            scalar_x(slot)
+            tensor_x(slot)
+            vector_x(slot)
+
         for half in range(2):
             widen(0, 2 * half)
             widen(0, 2 * half + 1)
             turn(0, half)
             leave(0, half)
+        make_table(0)
         permute_words(0, 0)
+        negate(0)
         quant_x(0, 0)
         permute_scales(0, 0)
-        negate(0)
         quant_x(0, 1)
         make_bias(0)
+        make_table(1)
+        early(-1)
 
         for blk in range(NB):
-            grp, j = divmod(blk, 4)
             new_planes(blk)
+            if blk > 0:
+                nc.vector.memset(inter[blk - 1][:, S_COLS : S_COLS + 4, :], 0.0)
+                zip_gp(blk - 1, S_COLS, TOK)
             for r in (1, 0, 3, 2):
                 project(blk, r)
                 rotate(blk, r)
-            if grp + 1 < GROUPS and j == 1:
-                for half in range(2):
-                    turn(grp + 1, half)
-                    leave(grp + 1, half)
+            tensor_x(blk)
+            scalar_x(blk)
+            for grp in range(GROUPS):
+                for b in range(2):
+                    if blk == 4 * grp + 6 + b:
+                        scores(grp, b)
+                        store(grp, b)
             if blk < NB - 1:
-                interleave(blk, 0, TOK, nc.scalar.copy)
+                interleave(blk, 0, S_COLS, nc.scalar.copy)
             if blk == 0:
-                make_table(1)
                 permute_words(0, 1)
                 permute_scales(0, 1)
                 make_bias(1)
@@ -328,23 +431,13 @@ def tile_ropeattention_pa_t_w4_kernel(
             if blk == 2:
                 permute_words(1, 1)
                 permute_scales(1, 1)
-            if blk > 0:
-                quant_qk(blk - 1, 0, TOK)
-            if grp + 1 < GROUPS:
-                if j == 0:
-                    for n in range(NT):
-                        widen(grp + 1, n)
-                if j == 2:
-                    quant_x(grp + 1, 0)
-                    negate(grp + 1)
-                    quant_x(grp + 1, 1)
-            if grp > 0 and j == 1:
-                scores(grp - 1, 0)
-            if grp > 0 and j == 2:
-                scores(grp - 1, 1)
-
+            if blk >= 2:
+                quant_qk(blk - 2, 0, TOK)
+            vector_x(blk)
+        quant_qk(NB - 2, 0, TOK)
         interleave(NB - 1, 0, S, nc.vector.tensor_copy)
         interleave(NB - 1, S, TOK, nc.scalar.copy)
         for b in range(2):
             quant_qk(NB - 1, b * S, (b + 1) * S)
             scores(GROUPS - 1, b)
+            store(GROUPS - 1, b)

@@ -16,17 +16,27 @@ ALU = mybir.AluOpType
 ACT = mybir.ActivationFunctionType
 
 P = 128
+PACK = 4
 B, S, D, H = 16, 256, 512, 1024
 HEAD = H // 2
-TOK = 512
+TOK = 2 * S
 GROUPS = B * S // TOK
-NT = TOK // P
-PASSES = H // 512
-BLOCKS = [(0, 0), (0, 1), (1, 0), (1, 1)]
-NB = 4 * GROUPS
-SCALAR_GROUPS = [1,2,3,4,5,6,7]
+TILES = TOK // P
+PASSES = H // (P * PACK)
+QUERY, KEY = 0, 1
+BLOCKS = [(QUERY, 0), (QUERY, 1), (KEY, 0), (KEY, 1)]
+LAST = len(BLOCKS) * GROUPS - 1
+PLANES = (1, 0, 3, 2)
+ZIP_SCALAR = 240
+TAIL_VECTOR = 160
+FIRST_VECTOR = 384
+FIRST_TILES = 3
+PLAN = dict(widen=(-9, -9), turn=-7, leave=(-7, -6, -5, -4), zip=(-4, -4), negate=-2, plus=-2, minus=-1)
+PLAN_1 = dict(widen=(), turn=0, leave=(1, 1, 1, 2), zip=(2, 2), negate=2, plus=2, minus=2)
+LAG = 2
+SCORES = 6
+NEG_SCALAR = [2, 4, 6, 7]
 
-S_COLS = 256
 FLOPS = 2 * B * S * D * 2 * H + 2 * B * S * S * H
 
 
@@ -36,59 +46,54 @@ def tile_ropeattention_pa_t_w4_kernel(
     nc = tc.nc
     with ExitStack() as ctx:
         keep = ctx.enter_context(tc.tile_pool(name="keep", bufs=1))
-        xin = ctx.enter_context(tc.tile_pool(name="xin", bufs=GROUPS))
         work = ctx.enter_context(tc.tile_pool(name="work", bufs=3))
         roll = ctx.enter_context(tc.tile_pool(name="roll", bufs=4))
-        ps_qk = ctx.enter_context(tc.psum_pool(name="ps_qk", bufs=5))
+        ps_proj = ctx.enter_context(tc.psum_pool(name="ps_proj", bufs=5))
         ps_aux = ctx.enter_context(tc.psum_pool(name="ps_aux", bufs=3))
         ctx.enter_context(tc.manual_schedule())
 
+        scale_col = keep.tile([P, PACK], F32)
+        nc.scalar.dma_start(out=scale_col[:], in_=hidden_scale.rearrange("a b (p t) -> p (a b t)", t=PACK))
+
         tokens = hidden_bytes.rearrange("b s k -> (b s) k")
-
-        scale_bc = keep.tile([P, D], F32)
-        nc.scalar.dma_start(out=scale_bc[:], in_=hidden_scale.rearrange("a b k -> (a b k)").partition_broadcast(P))
-
-        scale_col = keep.tile([P, 4], F32)
-        nc.scalar.dma_start(out=scale_col[:], in_=hidden_scale.rearrange("a b (p t) -> p (a b t)", t=4))
-
-        x_bytes = []
-        for grp in range(GROUPS):
-            xb = xin.tile([P, NT, D], U8, name="xb", align_bytes=64)
-            x_bytes.append(xb)
+        x_bytes = keep.tile([P, GROUPS, TILES, D], U8, align_bytes=64)
 
         def load_x(grp, n0, n1):
             rows = tokens[grp * TOK : (grp + 1) * TOK, :].rearrange("(n p) k -> p n k", p=P)
-            nc.sync.dma_start(out=x_bytes[grp][:, n0:n1, :], in_=rows[:, n0:n1, :])
+            nc.sync.dma_start(out=x_bytes[:, grp, n0:n1, :], in_=rows[:, n0:n1, :])
 
         load_x(0, 0, 2)
-        load_x(0, 2, 4)
-        wraw = keep.tile([P, 2, 2 * H], U8, align_bytes=64)
-        sraw = keep.tile([P, 2, H], U8, align_bytes=64)
-        nc.sync.dma_start(out=wraw[:, 0, :], in_=wq_words[0])
-        load_x(1, 0, NT)
+        load_x(0, 2, TILES)
+        w_raw = keep.tile([P, 2, 2 * H], U8, align_bytes=64)
+        s_raw = keep.tile([P, 2, H], U8, align_bytes=64)
+        nc.sync.dma_start(out=w_raw[:, QUERY, :], in_=wq_words[0])
 
         p_int = keep.tile([P, 1], I32)
         nc.gpsimd.iota(p_int[:], pattern=[[0, 1]], base=0, channel_multiplier=1)
+        nc.gpsimd.memset(s_raw[:].rearrange("p a n -> p (a n)").bitcast(I32), 0)
         s_f = keep.tile([P, S], F32)
         nc.gpsimd.iota(s_f[:], pattern=[[1, S]], base=0, channel_multiplier=0, allow_small_or_imprecise_dtypes=True)
-        nc.gpsimd.memset(sraw[:].rearrange("p a n -> p (a n)").bitcast(I32), 0)
         ident = keep.tile([P, P], F32)
         make_identity(nc, ident[:])
 
-        for i, s in enumerate((wq_scales, wk_scales)):
+        b_raw = []
+
+        def load_small(i, s, b):
             for q in range(4):
                 nc.sync.dma_start(
-                    out=sraw[32 * q : 32 * q + 4, i, :].bitcast(I32),
+                    out=s_raw[32 * q : 32 * q + 4, i, :].bitcast(I32),
                     in_=s[0, 4 * q : 4 * q + 4, :].bitcast(I32),
                 )
-        braw = []
-        for i, b in enumerate((bq, bk)):
-            br = keep.tile([P, PASSES, 4], BF16, name="br%d" % i)
-            nc.sync.dma_start(out=br[:], in_=b.rearrange("(g p r) -> p g r", p=P, r=4))
-            braw.append(br)
-        nc.sync.dma_start(out=wraw[:, 1, :], in_=wk_words[0])
+            br = keep.tile([P, PASSES, PACK], BF16, name="b_raw%d" % i)
+            nc.sync.dma_start(out=br[:], in_=b.rearrange("(g p r) -> p g r", p=P, r=PACK))
+            b_raw.append(br)
+
+        load_small(QUERY, wq_scales, bq)
+        load_x(1, 0, TILES)
+        nc.sync.dma_start(out=w_raw[:, KEY, :], in_=wk_words[0])
+        load_small(KEY, wk_scales, bk)
         for grp in range(2, GROUPS):
-            load_x(grp, 0, NT)
+            load_x(grp, 0, TILES)
 
         rho = 10000.0 ** (-1.0 / (HEAD // 2))
         bits = keep.tile([P, 7], I32)
@@ -111,27 +116,29 @@ def tile_ropeattention_pa_t_w4_kernel(
         nc.vector.tensor_tensor(out=f2[:, 1:2], in0=f3[:, 1:2], in1=f3[:, 2:3], op=ALU.mult)
         omega = keep.tile([P, 3], F32)
         nc.vector.tensor_tensor(out=omega[:, 0:1], in0=f2[:, 0:1], in1=f2[:, 1:2], op=ALU.mult)
-        nc.vector.tensor_scalar(
-            out=omega[:, 1:2], in0=omega[:, 0:1], scalar1=rho**P, scalar2=None, op0=ALU.mult
-        )
-        nc.vector.tensor_scalar(
-            out=omega[:, 2:3], in0=omega[:, 1:2], scalar1=-1.0, scalar2=None, op0=ALU.mult
-        )
         ang = keep.tile([P, S], F32)
         turns = keep.tile([P, S], I32)
         red1 = keep.tile([P, S], F32)
         red2 = keep.tile([P, S], F32)
         red3 = keep.tile([P, S], F32)
-        table = keep.tile([P, 4, TOK], F32)
+        table = keep.tile([P, 2 * PASSES, TOK], F32)
         c1 = 6.28125
         nc.vector.tensor_scalar(out=ang[:], in0=s_f[:], scalar1=omega[:, 0:1], scalar2=None, op0=ALU.mult)
         nc.vector.tensor_scalar(
+            out=omega[:, 1:2], in0=omega[:, 0:1], scalar1=rho**P, scalar2=None, op0=ALU.mult
+        )
+        nc.vector.tensor_scalar(
             out=turns[:], in0=ang[:], scalar1=1.0 / (2.0 * math.pi), scalar2=None, op0=ALU.mult
         )
-        nc.vector.scalar_tensor_tensor(out=red1[:], in0=turns[:], scalar=-c1, in1=ang[:], op0=ALU.mult, op1=ALU.add)
-        nc.vector.scalar_tensor_tensor(
-            out=red2[:], in0=turns[:], scalar=c1 - 2.0 * math.pi, in1=red1[:], op0=ALU.mult, op1=ALU.add
+        nc.vector.tensor_scalar(
+            out=omega[:, 2:3], in0=omega[:, 0:1], scalar1=-(rho**P), scalar2=None, op0=ALU.mult
         )
+        nc.vector.scalar_tensor_tensor(out=red1[:], in0=turns[:], scalar=-c1, in1=ang[:], op0=ALU.mult, op1=ALU.add)
+
+        def finish_angles():
+            nc.vector.scalar_tensor_tensor(
+                out=red2[:], in0=turns[:], scalar=c1 - 2.0 * math.pi, in1=red1[:], op0=ALU.mult, op1=ALU.add
+            )
 
         def make_table(g):
             if g == 0:
@@ -147,297 +154,296 @@ def tile_ropeattention_pa_t_w4_kernel(
                         out=table[:, 3, cols], in_=s_f[:], func=ACT.Sin, bias=half_pi[:], scale=omega[:, 2:3]
                     )
 
-        wperm = keep.tile([P, 2, PASSES, 4, 2 * P], U8, align_bytes=64)
-        sperm = keep.tile([P, 2, PASSES, 4, P], U8, align_bytes=64)
+        w_perm = keep.tile([P, 2, PASSES, PACK, 2 * P], U8, align_bytes=64)
+        s_perm = keep.tile([P, 2, PASSES, PACK, P], U8, align_bytes=64)
+        bias = keep.tile([P, 2, PASSES, PACK], F32)
 
-        def permute_words(i, g):
+        def sort_words(i, g):
+            n = 2 * P * PACK
             nc.vector.tensor_copy(
-                out=wperm[:, i, g].rearrange("p r (c b) -> p r c b", b=2),
-                in_=wraw[:, i, g * 1024 : (g + 1) * 1024].rearrange("p (c r b) -> p r c b", r=4, b=2),
+                out=w_perm[:, i, g].rearrange("p r (c b) -> p r c b", b=2),
+                in_=w_raw[:, i, g * n : (g + 1) * n].rearrange("p (c r b) -> p r c b", r=PACK, b=2),
             )
 
-        def permute_scales(i, g):
+        def sort_scales(i, g):
+            n = P * PACK
             nc.vector.tensor_copy(
-                out=sperm[:, i, g], in_=sraw[:, i, g * 512 : (g + 1) * 512].rearrange("p (c r) -> p r c", r=4)
+                out=s_perm[:, i, g], in_=s_raw[:, i, g * n : (g + 1) * n].rearrange("p (c r) -> p r c", r=PACK)
             )
-
-        x_wide = {}
-        x_tr = {}
-        x_grp = {}
-        x_neg = {}
-        x_pl = {}
-        sc_bank = {}
-        x_q = {}
-        qk_q = {}
-        planes = {}
-        inter = {}
-        lifted = {}
-        banks = {}
-
-        def widen(grp, n):
-            if n == 0:
-                xw = work.tile([P, NT, D], BF16, name="xw", align_bytes=64)
-                x_wide[grp] = xw
-            nc.vector.tensor_tensor(
-                out=x_wide[grp][:, n, :], in0=x_bytes[grp][:, n, :].bitcast(FP8), in1=scale_bc[:], op=ALU.mult
-            )
-
-        def widen_plain(grp, n0, n1):
-            if n0 == 0:
-                xw = work.tile([P, NT, D], BF16, name="xw", align_bytes=64)
-                x_wide[grp] = xw
-            nc.scalar.copy(
-                out=x_wide[grp][:, n0:n1, :].rearrange("p n k -> p (n k)"),
-                in_=x_bytes[grp][:, n0:n1, :].rearrange("p n k -> p (n k)").bitcast(FP8),
-            )
-
-        def turn(grp, half):
-            bank = ps_aux.tile([P, 2, 2, P], F32, name="bank_tr", tag="aux")
-            x_tr[grp, half] = bank
-            for n in range(2):
-                words = x_wide[grp][:, 2 * half + n, :].bitcast(F32)
-                for u in range(2):
-                    nc.tensor.transpose(bank[:, n, u, :], words[:, u : D // 2 : 2], ident[:])
-
-        def turn_plain(grp, u):
-            bank = ps_aux.tile([P, NT, P], F32, name="bank_tu", tag="aux")
-            x_tr[grp, u] = bank
-            for n in range(NT):
-                words = x_wide[grp][:, n, :].bitcast(F32)
-                nc.tensor.transpose(bank[:, n, :], words[:, u : D // 2 : 2], ident[:])
-
-        def new_xg(grp):
-            xg = work.tile([P, TOK, 4], BF16, name="xg", align_bytes=64)
-            x_grp[grp] = xg
-
-        def leave(grp, half):
-            if half == 0:
-                new_xg(grp)
-            words = x_grp[grp][:].rearrange("p t j -> p (t j)").bitcast(F32)
-            nc.scalar.copy(
-                out=words[:, half * 512 : (half + 1) * 512].rearrange("p (n r u) -> p n r u", n=2, u=2),
-                in_=x_tr[grp, half][:].rearrange("p n u r -> p n r u"),
-            )
-
-        def leave_scaled(grp, t):
-            if t == 0:
-                xp = work.tile([P, 4, TOK], BF16, name="xp", align_bytes=64)
-                x_pl[grp] = xp
-            u, e = divmod(t, 2)
-            pairs = x_tr[grp, u][:].rearrange("p n r -> p (n r)").bitcast(BF16).rearrange("p (c e) -> p c e", e=2)
-            nc.scalar.activation(
-                out=x_pl[grp][:, t, :], in_=pairs[:, :, e], func=ACT.Copy, scale=scale_col[:, t : t + 1]
-            )
-
-        def zip_x(grp, c0, c1):
-            if c0 == 0:
-                new_xg(grp)
-            nc.scalar.copy(
-                out=x_grp[grp][:, c0:c1, :].rearrange("p (c i) t -> p c t i", i=4),
-                in_=x_pl[grp][:, :, c0:c1].rearrange("p t (c i) -> p c t i", i=4),
-            )
-
-        def negate(grp):
-            xn = work.tile([P, TOK, 4], BF16, name="xn", align_bytes=64)
-            x_neg[grp] = xn
-            nc.vector.tensor_scalar(out=xn[:], in0=x_grp[grp][:], scalar1=-1.0, scalar2=None, op0=ALU.mult)
-
-        def quant_x(grp, sign):
-            codes = work.tile([P, TOK], U32, name="xc%d" % sign, align_bytes=64)
-            scales = work.tile([P, TOK], U8, name="xs%d" % sign, align_bytes=64)
-            x_q[grp, sign] = (codes, scales)
-            src = (x_grp if sign == 0 else x_neg)[grp]
-            nc.vector.quantize_mx(
-                out=codes[:].bitcast(FP8X4), scales=scales[:], in_=src[:].rearrange("p t j -> p (t j)")
-            )
-
-        bias = keep.tile([P, 2, PASSES, 4], F32)
 
         def make_bias(i):
-            raw = braw[i][:].rearrange("p g (h two) -> p (g h) two", two=2)
+            raw = b_raw[i][:].rearrange("p g (h two) -> p (g h) two", two=2)
             res = bias[:, i].rearrange("p g (h two) -> p (g h) two", two=2)
             nc.vector.tensor_tensor(out=res[:, :, 0], in0=raw[:, :, 0], in1=raw[:, :, 1], op=ALU.subtract)
             nc.vector.tensor_tensor(out=res[:, :, 1], in0=raw[:, :, 0], in1=raw[:, :, 1], op=ALU.add)
 
+        wide, turned, split, zipped, negated, x_codes = {}, {}, {}, {}, {}, {}
+
+        def new_wide(grp):
+            xw = work.tile([P, TILES, D], BF16, name="xw", align_bytes=64)
+            wide[grp] = xw
+
+        def new_zipped(grp):
+            xz = work.tile([P, TOK, PACK], BF16, name="xz", align_bytes=64)
+            zipped[grp] = xz
+
+        def widen(copy, grp, n0, n1):
+            copy(
+                out=wide[grp][:, n0:n1, :].rearrange("p n k -> p (n k)"),
+                in_=x_bytes[:, grp, n0:n1, :].rearrange("p n k -> p (n k)").bitcast(FP8),
+            )
+
+        def turn(grp, u):
+            bank = ps_aux.tile([P, TILES, P], F32, name="bank_turn", tag="aux")
+            turned[grp, u] = bank
+            for n in range(TILES):
+                words = wide[grp][:, n, :].bitcast(F32)
+                nc.tensor.transpose(bank[:, n, :], words[:, u : D // 2 : 2], ident[:])
+
+        def new_split(grp):
+            xs = work.tile([P, PACK, TOK], BF16, name="xs", align_bytes=64)
+            split[grp] = xs
+
+        def planes_of(grp, t):
+            u, e = divmod(t, 2)
+            pairs = turned[grp, u][:].rearrange("p n r -> p (n r)").bitcast(BF16).rearrange("p (c e) -> p c e", e=2)
+            return split[grp][:, t, :], pairs[:, :, e], scale_col[:, t : t + 1]
+
+        def leave_scalar(grp, t):
+            dst, src, factor = planes_of(grp, t)
+            nc.scalar.activation(out=dst, in_=src, func=ACT.Copy, scale=factor)
+
+        def leave_vector(grp, t):
+            dst, src, factor = planes_of(grp, t)
+            nc.vector.tensor_scalar(out=dst, in0=src, scalar1=factor, scalar2=None, op0=ALU.mult)
+
+        def zip_x(copy, grp, c0, c1):
+            copy(
+                out=zipped[grp][:, c0:c1, :].rearrange("p (c i) t -> p c t i", i=4),
+                in_=split[grp][:, :, c0:c1].rearrange("p t (c i) -> p c t i", i=4),
+            )
+
+        def negate(grp, eng):
+            xn = work.tile([P, TOK, PACK], BF16, name="xn", align_bytes=64)
+            negated[grp] = xn
+            if eng == "D":
+                nc.vector.tensor_scalar(out=xn[:], in0=zipped[grp][:], scalar1=-1.0, scalar2=None, op0=ALU.mult)
+            if eng == "S":
+                nc.scalar.activation(out=xn[:], in_=zipped[grp][:], func=ACT.Copy, scale=-1.0)
+
+        def quantize_x(grp, minus):
+            codes = work.tile([P, TOK], U32, name="x_codes%d" % minus, align_bytes=64)
+            scales = work.tile([P, TOK], U8, name="x_scales%d" % minus, align_bytes=64)
+            x_codes[grp, minus] = (codes, scales)
+            src = (negated if minus else zipped)[grp]
+            nc.vector.quantize_mx(
+                out=codes[:].bitcast(FP8X4), scales=scales[:], in_=src[:].rearrange("p c t -> p (c t)")
+            )
+
+        sums, rotated, ready, qk_codes, score_banks = {}, {}, {}, {}, {}
+
         def project(blk, r):
-            grp, j = divmod(blk, 4)
+            grp, j = divmod(blk, len(BLOCKS))
             i, g = BLOCKS[j]
-            acc = ps_qk.tile([P, TOK], F32, name="acc")
-            banks[blk, r] = acc
-            first = r // 2 * 2
-            for half in range(2):
-                sign = 1 if (half == 1 and r % 2 == 0) else 0
-                codes, scales = x_q[grp, sign]
+            acc = ps_proj.tile([P, TOK], F32, name="acc")
+            sums[blk, r] = acc
+            even = r // 2 * 2
+            for odd in range(2):
+                codes, scales = x_codes[grp, 1 if odd == 1 and r % 2 == 0 else 0]
                 nc.tensor.matmul_mx(
                     out=acc[:],
-                    lhsT=wperm[:, i, g, first + half, :].bitcast(FP4X4),
-                    lhsT_scale=sperm[:, i, g, first + half, :],
+                    lhsT=w_perm[:, i, g, even + odd, :].bitcast(FP4X4),
+                    lhsT_scale=s_perm[:, i, g, even + odd, :],
                     rhs=codes[:].bitcast(FP8X4),
                     rhs_scale=scales[:],
-                    start=(half == 0),
-                    stop=(half == 1),
+                    start=(odd == 0),
+                    stop=(odd == 1),
                 )
 
-        def new_planes(blk):
-            pl = roll.tile([P, 4, TOK], BF16, name="pl", align_bytes=64)
-            planes[blk] = pl
+        def new_rotated(blk):
+            rot = roll.tile([P, PACK, TOK], BF16, name="rot", align_bytes=64)
+            rotated[blk] = rot
 
-        def rotate(blk, r):
-            i, g = BLOCKS[blk % 4]
+        def rotate(blk, r, c0, c1):
+            i, g = BLOCKS[blk % len(BLOCKS)]
             nc.vector.scalar_tensor_tensor(
-                out=planes[blk][:, r, :], in0=banks[blk, r][:], scalar=bias[:, i, g, r : r + 1],
-                in1=table[:, 2 * g + r // 2, :], op0=ALU.add, op1=ALU.mult,
+                out=rotated[blk][:, r, c0:c1], in0=sums[blk, r][:, c0:c1], scalar=bias[:, i, g, r : r + 1],
+                in1=table[:, 2 * g + r // 2, c0:c1], op0=ALU.add, op1=ALU.mult,
             )
 
-        def interleave(blk, c0, c1, eng):
-            if c0 == 0:
-                qi = roll.tile([P, TOK, 4], BF16, name="qi", align_bytes=64)
-                inter[blk] = qi
-            eng(
-                out=inter[blk][:, c0:c1, :].rearrange("p (c i) t -> p c t i", i=4),
-                in_=planes[blk][:, :, c0:c1].rearrange("p t (c i) -> p c t i", i=4),
+        def new_ready(blk):
+            rdy = roll.tile([P, TOK, PACK], BF16, name="rdy", align_bytes=64)
+            ready[blk] = rdy
+
+        def zip_copy(copy, blk, c0, c1):
+            copy(
+                out=ready[blk][:, c0:c1, :].rearrange("p (c i) t -> p c t i", i=4),
+                in_=rotated[blk][:, :, c0:c1].rearrange("p t (c i) -> p c t i", i=4),
             )
 
-        def zip_gp(blk, c0, c1):
+        def mark_ready(blk, c0):
+            nc.vector.memset(ready[blk][:, c0 : c0 + 4, :], 0.0)
+
+        def zip_gpsimd(blk, c0, c1):
             nc.gpsimd.tensor_scalar(
-                out=inter[blk][:, c0:c1, :], in0=planes[blk][:, :, c0:c1].rearrange("p t c -> p c t"),
+                out=ready[blk][:, c0:c1, :], in0=rotated[blk][:, :, c0:c1].rearrange("p t c -> p c t"),
                 scalar1=1.0, scalar2=1.0, op0=ALU.mult, op1=ALU.mult,
             )
 
-        def quant_qk(blk, c0, c1):
-            j = blk % 4
+        def quantize_qk(blk, c0, c1):
+            j = blk % len(BLOCKS)
             if c0 == 0:
-                codes = roll.tile([P, TOK], U32, name="qc%d" % j, align_bytes=64)
-                scales = roll.tile([P, TOK], U8, name="qs%d" % j, align_bytes=64)
-                qk_q[blk] = (codes, scales)
-            codes, scales = qk_q[blk]
+                codes = roll.tile([P, TOK], U32, name="codes%d" % j, align_bytes=64)
+                scales = roll.tile([P, TOK], U8, name="scales%d" % j, align_bytes=64)
+                qk_codes[blk] = (codes, scales)
+            codes, scales = qk_codes[blk]
             nc.vector.quantize_mx(
                 out=codes[:, c0:c1].bitcast(FP8X4), scales=scales[:, c0:c1],
-                in_=inter[blk][:, c0:c1, :].rearrange("p t j -> p (t j)"),
+                in_=ready[blk][:, c0:c1, :].rearrange("p c t -> p (c t)"),
             )
 
+        def score(grp, b, m, bank):
+            rows = slice(b * S + m * P, b * S + (m + 1) * P)
+            cols = slice(b * S, (b + 1) * S)
+            for g in range(PASSES):
+                q_codes, q_scales = qk_codes[len(BLOCKS) * grp + g]
+                k_codes, k_scales = qk_codes[len(BLOCKS) * grp + PASSES + g]
+                nc.tensor.matmul_mx(
+                    out=bank,
+                    lhsT=q_codes[:, rows].bitcast(FP8X4), lhsT_scale=q_scales[:, rows],
+                    rhs=k_codes[:, cols].bitcast(FP8X4), rhs_scale=k_scales[:, cols],
+                    start=(g == 0), stop=(g == PASSES - 1),
+                )
+
+        root = 1.0 / math.sqrt(HEAD)
+
         def scores(grp, b):
-            sc = ps_aux.tile([P, 2, S], F32, name="sc", tag="aux")
-            sc_bank[grp, b] = sc
+            bank = ps_aux.tile([P, 2, S], F32, name="bank_score", tag="aux")
+            score_banks[grp, b] = bank
             for m in range(2):
-                for g in range(PASSES):
-                    qcod, qsc = qk_q[4 * grp + g]
-                    kcod, ksc = qk_q[4 * grp + PASSES + g]
-                    rows = slice(b * S + m * P, b * S + (m + 1) * P)
-                    cols = slice(b * S, (b + 1) * S)
-                    nc.tensor.matmul_mx(
-                        out=sc[:, m, :],
-                        lhsT=qcod[:, rows].bitcast(FP8X4), lhsT_scale=qsc[:, rows],
-                        rhs=kcod[:, cols].bitcast(FP8X4), rhs_scale=ksc[:, cols],
-                        start=(g == 0), stop=(g == PASSES - 1),
-                    )
+                score(grp, b, m, bank[:, m, :])
 
         def store(grp, b):
             res = roll.tile([P, 2, S], F32, name="res")
-            nc.scalar.activation(out=res[:], in_=sc_bank[grp, b][:], func=ACT.Copy, scale=1.0 / math.sqrt(HEAD))
-            nc.sync.dma_start(out=out[grp * 2 + b].rearrange("(m p) n -> p m n", p=P), in_=res[:])
+            nc.scalar.activation(out=res[:], in_=score_banks[grp, b][:], func=ACT.Copy, scale=root)
+            nc.sync.dma_start(out=out[2 * grp + b].rearrange("(m p) n -> p m n", p=P), in_=res[:])
 
-        XI = dict(wp0=-9, wp1=-8, t=-7, l0=-6, l1=-6, l2=-5, l3=-5, z0=-4, z1=-3, neg=-2, q0=-2, q1=-2)
-        X4 = dict(w0=-8, w1=-8, w2=-7, w3=-6, t0=-6, t1=-5, l0=-5, l1=-4, neg=-3, q0=-3, q1=-2)
-        XI1 = dict(wp0=-1, wp1=-1, t=0, l0=0, l1=0, l2=1, l3=1, z0=2, z1=2, neg=2, q0=2, q1=2)
-        X41 = dict(w0=-1, w1=-1, w2=0, w3=0, t0=0, t1=1, l0=1, l1=1, neg=2, q0=2, q1=2)
-
-        def steps(slot, which):
+        def due(slot, step):
+            res = []
             for grp in range(1, GROUPS):
-                scal = grp in SCALAR_GROUPS
-                plan = (XI1 if scal else X41) if grp == 1 else (XI if scal else X4)
-                shift = 0 if grp == 1 else 4 * grp
-                for key in plan:
-                    if max(plan[key] + shift, -1) == slot:
-                        which(grp, scal, key)
+                plan = PLAN_1 if grp == 1 else PLAN
+                base = 0 if grp == 1 else len(BLOCKS) * grp
+                when = plan[step]
+                for part, w in enumerate(when if isinstance(when, tuple) else (when,)):
+                    if max(base + w, 0) == slot:
+                        res.append((grp, part))
+            return res
 
-        def scalar_step(grp, scal, key):
-            if key in ("wp0", "wp1"):
-                n = 2 * int(key[2])
-                widen_plain(grp, n, n + 2)
-            elif key[0] == "l":
-                (leave_scaled if scal else leave)(grp, int(key[1]))
-            elif key[0] == "z":
-                zip_x(grp, S * int(key[1]), S * (int(key[1]) + 1))
+        def prepare_tensor(slot):
+            for grp, part in due(slot, "turn"):
+                turn(grp, 0)
+                turn(grp, 1)
 
-        def tensor_step(grp, scal, key):
-            if key == "t":
-                turn_plain(grp, 0)
-                turn_plain(grp, 1)
-            elif key[0] == "t":
-                turn(grp, int(key[1]))
+        def prepare_scalar(slot):
+            for grp, part in due(slot, "widen"):
+                if part == 0:
+                    new_wide(grp)
+                widen(nc.scalar.copy, grp, 2 * part, 2 * part + 2)
+            for grp, part in due(slot, "leave"):
+                if part == 0:
+                    new_split(grp)
+                leave_scalar(grp, part)
+            for grp, part in due(slot, "zip"):
+                if part == 0:
+                    new_zipped(grp)
+                zip_x(nc.scalar.copy, grp, S * part, S * (part + 1))
+            for grp, part in due(slot, "negate"):
+                if grp in NEG_SCALAR:
+                    negate(grp, "S")
 
-        def vector_step(grp, scal, key):
-            if key[0] == "w" and not scal:
-                widen(grp, int(key[1]))
-            elif key == "neg":
-                negate(grp)
-            elif key[0] == "q":
-                quant_x(grp, int(key[1]))
+        def prepare_vector(slot):
+            for grp, part in due(slot, "negate"):
+                if grp not in NEG_SCALAR:
+                    negate(grp, "D")
+            for grp, part in due(slot, "plus"):
+                quantize_x(grp, 0)
+            for grp, part in due(slot, "minus"):
+                quantize_x(grp, 1)
 
-        def scalar_x(slot):
-            steps(slot, scalar_step)
-
-        def tensor_x(slot):
-            steps(slot, tensor_step)
-
-        def vector_x(slot):
-            steps(slot, vector_step)
-
-        def early(slot):
-            scalar_x(slot)
-            tensor_x(slot)
-            vector_x(slot)
-
-        for half in range(2):
-            widen(0, 2 * half)
-            widen(0, 2 * half + 1)
-            turn(0, half)
-            leave(0, half)
+        new_wide(0)
+        for n in range(FIRST_TILES):
+            widen(nc.vector.tensor_copy, 0, n, n + 1)
+        for n in range(FIRST_TILES, TILES):
+            widen(nc.scalar.copy, 0, n, n + 1)
+        turn(0, 0)
+        turn(0, 1)
+        finish_angles()
+        sort_words(QUERY, 0)
+        new_split(0)
+        for t in (0, 1):
+            leave_scalar(0, t)
+        for t in (2, 3):
+            leave_vector(0, t)
+        new_zipped(0)
+        sort_scales(QUERY, 0)
+        zip_x(nc.vector.tensor_copy, 0, 0, FIRST_VECTOR)
+        zip_x(nc.scalar.copy, 0, FIRST_VECTOR, TOK)
         make_table(0)
-        permute_words(0, 0)
-        negate(0)
-        quant_x(0, 0)
-        permute_scales(0, 0)
-        quant_x(0, 1)
-        make_bias(0)
+        quantize_x(0, 0)
+        negate(0, "D")
+        make_bias(QUERY)
+        quantize_x(0, 1)
+        new_wide(1)
+        widen(nc.scalar.copy, 1, 0, TILES)
         make_table(1)
-        early(-1)
 
-        for blk in range(NB):
-            new_planes(blk)
+        for blk in range(LAST + 1):
+            new_rotated(blk)
             if blk > 0:
-                nc.vector.memset(inter[blk - 1][:, S_COLS : S_COLS + 4, :], 0.0)
-                zip_gp(blk - 1, S_COLS, TOK)
-            for r in (1, 0, 3, 2):
+                mark_ready(blk - 1, ZIP_SCALAR)
+                zip_gpsimd(blk - 1, ZIP_SCALAR, TOK)
+            for r in PLANES:
                 project(blk, r)
-                rotate(blk, r)
-            tensor_x(blk)
-            scalar_x(blk)
+                if blk < LAST:
+                    rotate(blk, r, 0, TOK)
+            if blk == LAST:
+                for b in range(2):
+                    for r in PLANES:
+                        rotate(blk, r, b * S, (b + 1) * S)
+            prepare_tensor(blk)
+            prepare_scalar(blk)
             for grp in range(GROUPS):
                 for b in range(2):
-                    if blk == 4 * grp + 6 + b:
+                    if blk == len(BLOCKS) * grp + SCORES + b:
                         scores(grp, b)
                         store(grp, b)
-            if blk < NB - 1:
-                interleave(blk, 0, S_COLS, nc.scalar.copy)
-            if blk == 0:
-                permute_words(0, 1)
-                permute_scales(0, 1)
-                make_bias(1)
+            new_ready(blk)
+            if blk < LAST:
+                zip_copy(nc.scalar.copy, blk, 0, ZIP_SCALAR)
+            if blk < 3:
+                sort_words(*BLOCKS[blk + 1])
+                sort_scales(*BLOCKS[blk + 1])
             if blk == 1:
-                permute_words(1, 0)
-                permute_scales(1, 0)
-            if blk == 2:
-                permute_words(1, 1)
-                permute_scales(1, 1)
-            if blk >= 2:
-                quant_qk(blk - 2, 0, TOK)
-            vector_x(blk)
-        quant_qk(NB - 2, 0, TOK)
-        interleave(NB - 1, 0, S, nc.vector.tensor_copy)
-        interleave(NB - 1, S, TOK, nc.scalar.copy)
-        for b in range(2):
-            quant_qk(NB - 1, b * S, (b + 1) * S)
-            scores(GROUPS - 1, b)
-            store(GROUPS - 1, b)
+                make_bias(KEY)
+            if blk >= LAG:
+                quantize_qk(blk - LAG, 0, TOK)
+            prepare_vector(blk)
+        zip_copy(nc.scalar.copy, LAST, 0, S)
+        zip_copy(nc.vector.tensor_copy, LAST, S, S + TAIL_VECTOR)
+        zip_copy(nc.scalar.copy, LAST, S + TAIL_VECTOR, TOK)
+        for back in range(LAG - 1, 0, -1):
+            quantize_qk(LAST - back, 0, TOK)
+        quantize_qk(LAST, 0, S)
+        scores(GROUPS - 1, 0)
+        quantize_qk(LAST, S, TOK)
+        ends = []
+        for m in range(2):
+            bank = ps_aux.tile([P, S], F32, name="bank_end%d" % m, tag="aux")
+            score(GROUPS - 1, 1, m, bank[:])
+            ends.append(bank)
+        res = roll.tile([P, 2, S], F32, name="res_end")
+        store(GROUPS - 1, 0)
+        nc.vector.tensor_scalar(out=res[:, 0, :], in0=ends[0][:], scalar1=root, scalar2=None, op0=ALU.mult)
+        nc.sync.dma_start(out=out[B - 1, 0:P, :], in_=res[:, 0, :])
+        nc.scalar.activation(out=res[:, 1, :], in_=ends[1][:], func=ACT.Copy, scale=root)
+        nc.sync.dma_start(out=out[B - 1, P:S, :], in_=res[:, 1, :])

@@ -17,8 +17,10 @@ ACT = mybir.ActivationFunctionType
 
 P = 128
 PACK = 4
+WORD4 = 2
 B, S, D, H = 16, 256, 512, 1024
 HEAD = H // 2
+ANGLES = H // 4
 TOK = 2 * S
 GROUPS = B * S // TOK
 TILES = TOK // P
@@ -26,16 +28,19 @@ PASSES = H // (P * PACK)
 QUERY, KEY = 0, 1
 BLOCKS = [(QUERY, 0), (QUERY, 1), (KEY, 0), (KEY, 1)]
 LAST = len(BLOCKS) * GROUPS - 1
-PLANES = (1, 0, 3, 2)
+PLANES = (1, 3, 0, 2)
+BITS = 7
+
 ZIP_SCALAR = 240
-TAIL_VECTOR = 160
-FIRST_VECTOR = 384
-FIRST_TILES = 3
-PLAN = dict(widen=(-9, -9), turn=-7, leave=(-7, -6, -5, -4), zip=(-4, -4), negate=-2, plus=-2, minus=-1)
-PLAN_1 = dict(widen=(), turn=0, leave=(1, 1, 1, 2), zip=(2, 2), negate=2, plus=2, minus=2)
-LAG = 2
-SCORES = 6
-NEG_SCALAR = [2, 4, 6, 7]
+FIRST_TILES = 2
+FIRST_ZIP = 352
+TAIL_ZIP = 160
+NEGATED_BY_SCALAR = (2, 4, 6, 7)
+
+PLAN = dict(widen=(-10, -9), turn=(-7,), leave=(-7, -6, -6, -5), zip=(-5, -4), negate=(-3,), plus=(-3,), minus=(-2,))
+PLAN_1 = dict(widen=(), turn=(-4,), leave=(-4, -4, -4, -4), zip=(-3, -3), negate=(-2,), plus=(-2,), minus=(-2,))
+QUANTIZE_AFTER = 2
+SCORES_AFTER = 7
 
 FLOPS = 2 * B * S * D * 2 * H + 2 * B * S * S * H
 
@@ -47,7 +52,7 @@ def tile_ropeattention_pa_t_w4_kernel(
     with ExitStack() as ctx:
         keep = ctx.enter_context(tc.tile_pool(name="keep", bufs=1))
         work = ctx.enter_context(tc.tile_pool(name="work", bufs=3))
-        roll = ctx.enter_context(tc.tile_pool(name="roll", bufs=4))
+        roll = ctx.enter_context(tc.tile_pool(name="roll", bufs=5))
         ps_proj = ctx.enter_context(tc.psum_pool(name="ps_proj", bufs=5))
         ps_aux = ctx.enter_context(tc.psum_pool(name="ps_aux", bufs=3))
         ctx.enter_context(tc.manual_schedule())
@@ -64,105 +69,98 @@ def tile_ropeattention_pa_t_w4_kernel(
 
         load_x(0, 0, 2)
         load_x(0, 2, TILES)
-        w_raw = keep.tile([P, 2, 2 * H], U8, align_bytes=64)
+        load_x(1, 0, TILES)
+        w_raw = keep.tile([P, 2, WORD4 * H], U8, align_bytes=64)
         s_raw = keep.tile([P, 2, H], U8, align_bytes=64)
         nc.sync.dma_start(out=w_raw[:, QUERY, :], in_=wq_words[0])
 
-        p_int = keep.tile([P, 1], I32)
-        nc.gpsimd.iota(p_int[:], pattern=[[0, 1]], base=0, channel_multiplier=1)
-        nc.gpsimd.memset(s_raw[:].rearrange("p a n -> p (a n)").bitcast(I32), 0)
-        s_f = keep.tile([P, S], F32)
-        nc.gpsimd.iota(s_f[:], pattern=[[1, S]], base=0, channel_multiplier=0, allow_small_or_imprecise_dtypes=True)
+        one = keep.tile([P, 1], F32)
+        nc.vector.memset(one[:], 1.0)
+        warm = keep.tile([P, 1], F32)
+        nc.scalar.activation(out=warm[:], in_=one[:], func=ACT.Sin)
+        nc.vector.memset(s_raw[:].rearrange("p a n -> p (a n)").bitcast(I32), 0)
+        part_no = keep.tile([P, BITS], I32)
+        nc.gpsimd.iota(part_no[:], pattern=[[0, BITS]], base=0, channel_multiplier=1)
+        position = keep.tile([P, S], F32)
+        nc.gpsimd.iota(
+            position[:], pattern=[[1, S]], base=0, channel_multiplier=0, allow_small_or_imprecise_dtypes=True
+        )
         ident = keep.tile([P, P], F32)
         make_identity(nc, ident[:])
 
         b_raw = []
 
-        def load_small(i, s, b):
+        def load_scales_and_bias(i, s, b):
             for q in range(4):
                 nc.sync.dma_start(
-                    out=s_raw[32 * q : 32 * q + 4, i, :].bitcast(I32),
-                    in_=s[0, 4 * q : 4 * q + 4, :].bitcast(I32),
+                    out=s_raw[32 * q : 32 * q + 4, i, :].bitcast(I32), in_=s[0, 4 * q : 4 * q + 4, :].bitcast(I32)
                 )
             br = keep.tile([P, PASSES, PACK], BF16, name="b_raw%d" % i)
             nc.sync.dma_start(out=br[:], in_=b.rearrange("(g p r) -> p g r", p=P, r=PACK))
             b_raw.append(br)
 
-        load_small(QUERY, wq_scales, bq)
-        load_x(1, 0, TILES)
+        load_scales_and_bias(QUERY, wq_scales, bq)
         nc.sync.dma_start(out=w_raw[:, KEY, :], in_=wk_words[0])
-        load_small(KEY, wk_scales, bk)
+        load_scales_and_bias(KEY, wk_scales, bk)
         for grp in range(2, GROUPS):
             load_x(grp, 0, TILES)
 
-        rho = 10000.0 ** (-1.0 / (HEAD // 2))
-        bits = keep.tile([P, 7], I32)
-        fac = keep.tile([P, 7], F32)
-        for b in range(7):
-            nc.vector.tensor_single_scalar(out=bits[:, b : b + 1], in_=p_int[:], scalar=1 << b, op=ALU.bitwise_and)
-        half_pi = keep.tile([P, 1], F32)
-        nc.vector.tensor_scalar(
-            out=half_pi[:], in0=p_int[:], scalar1=0.0, scalar2=math.pi / 2.0, op0=ALU.mult, op1=ALU.add
-        )
-        for b in range(7):
+        rho = 10000.0 ** (-1.0 / ANGLES)
+        mask = keep.tile([P, BITS], I32)
+        for b in range(BITS):
+            nc.vector.memset(mask[:, b : b + 1], 1 << b)
+        slope = keep.tile([P, BITS], F32)
+        for b in range(BITS):
             nc.vector.tensor_scalar(
-                out=fac[:, b : b + 1], in0=bits[:, b : b + 1],
-                scalar1=(rho ** (1 << b) - 1.0) / (1 << b), scalar2=1.0, op0=ALU.mult, op1=ALU.add,
+                out=slope[:, b : b + 1], in0=one[:], scalar1=(rho ** (1 << b) - 1.0) / (1 << b), scalar2=None,
+                op0=ALU.mult,
             )
-        f3 = keep.tile([P, 3], F32)
-        nc.vector.tensor_tensor(out=f3[:], in0=fac[:, 0:3], in1=fac[:, 3:6], op=ALU.mult)
-        f2 = keep.tile([P, 2], F32)
-        nc.vector.tensor_tensor(out=f2[:, 0:1], in0=f3[:, 0:1], in1=fac[:, 6:7], op=ALU.mult)
-        nc.vector.tensor_tensor(out=f2[:, 1:2], in0=f3[:, 1:2], in1=f3[:, 2:3], op=ALU.mult)
+        half_pi = keep.tile([P, 1], F32)
+        nc.vector.tensor_scalar(out=half_pi[:], in0=one[:], scalar1=math.pi / 2.0, scalar2=None, op0=ALU.mult)
+        bits = keep.tile([P, BITS], I32)
+        nc.vector.tensor_tensor(out=bits[:], in0=part_no[:], in1=mask[:], op=ALU.bitwise_and)
+        step = keep.tile([P, BITS], F32)
+        nc.vector.tensor_tensor(out=step[:], in0=bits[:], in1=slope[:], op=ALU.mult)
+        factor = keep.tile([P, BITS], F32)
+        nc.vector.tensor_scalar(out=factor[:], in0=step[:], scalar1=1.0, scalar2=None, op0=ALU.add)
+
+        factor3 = keep.tile([P, 3], F32)
+        factor2 = keep.tile([P, 2], F32)
         omega = keep.tile([P, 3], F32)
-        nc.vector.tensor_tensor(out=omega[:, 0:1], in0=f2[:, 0:1], in1=f2[:, 1:2], op=ALU.mult)
-        ang = keep.tile([P, S], F32)
+        angle = keep.tile([P, S], F32)
         turns = keep.tile([P, S], I32)
-        red1 = keep.tile([P, S], F32)
-        red2 = keep.tile([P, S], F32)
-        red3 = keep.tile([P, S], F32)
+        reduced1 = keep.tile([P, S], F32)
+        reduced2 = keep.tile([P, S], F32)
+        reduced_abs = keep.tile([P, S], F32)
         table = keep.tile([P, 2 * PASSES, TOK], F32)
-        c1 = 6.28125
-        nc.vector.tensor_scalar(out=ang[:], in0=s_f[:], scalar1=omega[:, 0:1], scalar2=None, op0=ALU.mult)
-        nc.vector.tensor_scalar(
-            out=omega[:, 1:2], in0=omega[:, 0:1], scalar1=rho**P, scalar2=None, op0=ALU.mult
-        )
-        nc.vector.tensor_scalar(
-            out=turns[:], in0=ang[:], scalar1=1.0 / (2.0 * math.pi), scalar2=None, op0=ALU.mult
-        )
-        nc.vector.tensor_scalar(
-            out=omega[:, 2:3], in0=omega[:, 0:1], scalar1=-(rho**P), scalar2=None, op0=ALU.mult
-        )
-        nc.vector.scalar_tensor_tensor(out=red1[:], in0=turns[:], scalar=-c1, in1=ang[:], op0=ALU.mult, op1=ALU.add)
+        coarse = 6.28125
 
-        def finish_angles():
-            nc.vector.scalar_tensor_tensor(
-                out=red2[:], in0=turns[:], scalar=c1 - 2.0 * math.pi, in1=red1[:], op0=ALU.mult, op1=ALU.add
-            )
+        def table_0():
+            nc.scalar.activation(out=reduced_abs[:], in_=reduced2[:], func=ACT.Abs)
+            for b in range(TOK // S):
+                cols = slice(b * S, (b + 1) * S)
+                nc.scalar.activation(out=table[:, 0, cols], in_=reduced2[:], func=ACT.Sin)
+                nc.scalar.activation(
+                    out=table[:, 1, cols], in_=reduced_abs[:], func=ACT.Sin, bias=half_pi[:], scale=-1.0
+                )
 
-        def make_table(g):
-            if g == 0:
-                nc.scalar.activation(out=red3[:], in_=red2[:], func=ACT.Abs)
-            for rep in range(TOK // S):
-                cols = slice(rep * S, (rep + 1) * S)
-                if g == 0:
-                    nc.scalar.activation(out=table[:, 0, cols], in_=red2[:], func=ACT.Sin)
-                    nc.scalar.activation(out=table[:, 1, cols], in_=red3[:], func=ACT.Sin, bias=half_pi[:], scale=-1.0)
-                else:
-                    nc.scalar.activation(out=table[:, 2, cols], in_=s_f[:], func=ACT.Sin, scale=omega[:, 1:2])
-                    nc.scalar.activation(
-                        out=table[:, 3, cols], in_=s_f[:], func=ACT.Sin, bias=half_pi[:], scale=omega[:, 2:3]
-                    )
+        def table_1():
+            for b in range(TOK // S):
+                cols = slice(b * S, (b + 1) * S)
+                nc.scalar.activation(out=table[:, 2, cols], in_=position[:], func=ACT.Sin, scale=omega[:, 1:2])
+                nc.scalar.activation(
+                    out=table[:, 3, cols], in_=position[:], func=ACT.Sin, bias=half_pi[:], scale=omega[:, 2:3]
+                )
 
-        w_perm = keep.tile([P, 2, PASSES, PACK, 2 * P], U8, align_bytes=64)
+        w_perm = keep.tile([P, 2, PASSES, PACK, WORD4 * P], U8, align_bytes=64)
         s_perm = keep.tile([P, 2, PASSES, PACK, P], U8, align_bytes=64)
         bias = keep.tile([P, 2, PASSES, PACK], F32)
 
         def sort_words(i, g):
-            n = 2 * P * PACK
+            n = WORD4 * P * PACK
             nc.vector.tensor_copy(
-                out=w_perm[:, i, g].rearrange("p r (c b) -> p r c b", b=2),
-                in_=w_raw[:, i, g * n : (g + 1) * n].rearrange("p (c r b) -> p r c b", r=PACK, b=2),
+                out=w_perm[:, i, g].rearrange("p r (c b) -> p r c b", b=WORD4),
+                in_=w_raw[:, i, g * n : (g + 1) * n].rearrange("p (c r b) -> p r c b", r=PACK, b=WORD4),
             )
 
         def sort_scales(i, g):
@@ -183,10 +181,6 @@ def tile_ropeattention_pa_t_w4_kernel(
             xw = work.tile([P, TILES, D], BF16, name="xw", align_bytes=64)
             wide[grp] = xw
 
-        def new_zipped(grp):
-            xz = work.tile([P, TOK, PACK], BF16, name="xz", align_bytes=64)
-            zipped[grp] = xz
-
         def widen(copy, grp, n0, n1):
             copy(
                 out=wide[grp][:, n0:n1, :].rearrange("p n k -> p (n k)"),
@@ -204,32 +198,37 @@ def tile_ropeattention_pa_t_w4_kernel(
             xs = work.tile([P, PACK, TOK], BF16, name="xs", align_bytes=64)
             split[grp] = xs
 
-        def planes_of(grp, t):
+        def leave_operands(grp, t):
             u, e = divmod(t, 2)
-            pairs = turned[grp, u][:].rearrange("p n r -> p (n r)").bitcast(BF16).rearrange("p (c e) -> p c e", e=2)
-            return split[grp][:, t, :], pairs[:, :, e], scale_col[:, t : t + 1]
+            words = turned[grp, u][:].rearrange("p n c -> p (n c)")
+            halves = words.bitcast(BF16).rearrange("p (c e) -> p c e", e=2)
+            return split[grp][:, t, :], halves[:, :, e], scale_col[:, t : t + 1]
 
         def leave_scalar(grp, t):
-            dst, src, factor = planes_of(grp, t)
-            nc.scalar.activation(out=dst, in_=src, func=ACT.Copy, scale=factor)
+            dst, src, scale = leave_operands(grp, t)
+            nc.scalar.activation(out=dst, in_=src, func=ACT.Copy, scale=scale)
 
         def leave_vector(grp, t):
-            dst, src, factor = planes_of(grp, t)
-            nc.vector.tensor_scalar(out=dst, in0=src, scalar1=factor, scalar2=None, op0=ALU.mult)
+            dst, src, scale = leave_operands(grp, t)
+            nc.vector.tensor_scalar(out=dst, in0=src, scalar1=scale, scalar2=None, op0=ALU.mult)
 
-        def zip_x(copy, grp, c0, c1):
+        def zip_planes(copy, dst, src, c0, c1):
             copy(
-                out=zipped[grp][:, c0:c1, :].rearrange("p (c i) t -> p c t i", i=4),
-                in_=split[grp][:, :, c0:c1].rearrange("p t (c i) -> p c t i", i=4),
+                out=dst[:, c0:c1, :].rearrange("p (c i) t -> p c t i", i=4),
+                in_=src[:, :, c0:c1].rearrange("p t (c i) -> p c t i", i=4),
             )
 
-        def negate(grp, eng):
+        def new_zipped(grp):
+            xz = work.tile([P, TOK, PACK], BF16, name="xz", align_bytes=64)
+            zipped[grp] = xz
+
+        def negate(grp):
             xn = work.tile([P, TOK, PACK], BF16, name="xn", align_bytes=64)
             negated[grp] = xn
-            if eng == "D":
-                nc.vector.tensor_scalar(out=xn[:], in0=zipped[grp][:], scalar1=-1.0, scalar2=None, op0=ALU.mult)
-            if eng == "S":
+            if grp in NEGATED_BY_SCALAR:
                 nc.scalar.activation(out=xn[:], in_=zipped[grp][:], func=ACT.Copy, scale=-1.0)
+            else:
+                nc.vector.tensor_scalar(out=xn[:], in0=zipped[grp][:], scalar1=-1.0, scalar2=None, op0=ALU.mult)
 
         def quantize_x(grp, minus):
             codes = work.tile([P, TOK], U32, name="x_codes%d" % minus, align_bytes=64)
@@ -249,7 +248,8 @@ def tile_ropeattention_pa_t_w4_kernel(
             sums[blk, r] = acc
             even = r // 2 * 2
             for odd in range(2):
-                codes, scales = x_codes[grp, 1 if odd == 1 and r % 2 == 0 else 0]
+                minus = 1 if odd == 1 and r % 2 == 0 else 0
+                codes, scales = x_codes[grp, minus]
                 nc.tensor.matmul_mx(
                     out=acc[:],
                     lhsT=w_perm[:, i, g, even + odd, :].bitcast(FP4X4),
@@ -275,30 +275,24 @@ def tile_ropeattention_pa_t_w4_kernel(
             rdy = roll.tile([P, TOK, PACK], BF16, name="rdy", align_bytes=64)
             ready[blk] = rdy
 
-        def zip_copy(copy, blk, c0, c1):
-            copy(
-                out=ready[blk][:, c0:c1, :].rearrange("p (c i) t -> p c t i", i=4),
-                in_=rotated[blk][:, :, c0:c1].rearrange("p t (c i) -> p c t i", i=4),
-            )
-
-        def mark_ready(blk, c0):
-            nc.vector.memset(ready[blk][:, c0 : c0 + 4, :], 0.0)
-
-        def zip_gpsimd(blk, c0, c1):
+        def zip_gpsimd(blk):
+            nc.vector.memset(ready[blk][:, ZIP_SCALAR : ZIP_SCALAR + PACK, :], 0.0)
             nc.gpsimd.tensor_scalar(
-                out=ready[blk][:, c0:c1, :], in0=rotated[blk][:, :, c0:c1].rearrange("p t c -> p c t"),
+                out=ready[blk][:, ZIP_SCALAR:TOK, :],
+                in0=rotated[blk][:, :, ZIP_SCALAR:TOK].rearrange("p t c -> p c t"),
                 scalar1=1.0, scalar2=1.0, op0=ALU.mult, op1=ALU.mult,
             )
 
         def quantize_qk(blk, c0, c1):
-            j = blk % len(BLOCKS)
             if c0 == 0:
-                codes = roll.tile([P, TOK], U32, name="codes%d" % j, align_bytes=64)
-                scales = roll.tile([P, TOK], U8, name="scales%d" % j, align_bytes=64)
-                qk_codes[blk] = (codes, scales)
+                j = blk % len(BLOCKS)
+                new_codes = roll.tile([P, TOK], U32, name="codes%d" % j, align_bytes=64)
+                new_scales = roll.tile([P, TOK], U8, name="scales%d" % j, align_bytes=64)
+                qk_codes[blk] = (new_codes, new_scales)
             codes, scales = qk_codes[blk]
             nc.vector.quantize_mx(
-                out=codes[:, c0:c1].bitcast(FP8X4), scales=scales[:, c0:c1],
+                out=codes[:, c0:c1].bitcast(FP8X4),
+                scales=scales[:, c0:c1],
                 in_=ready[blk][:, c0:c1, :].rearrange("p c t -> p (c t)"),
             )
 
@@ -310,9 +304,12 @@ def tile_ropeattention_pa_t_w4_kernel(
                 k_codes, k_scales = qk_codes[len(BLOCKS) * grp + PASSES + g]
                 nc.tensor.matmul_mx(
                     out=bank,
-                    lhsT=q_codes[:, rows].bitcast(FP8X4), lhsT_scale=q_scales[:, rows],
-                    rhs=k_codes[:, cols].bitcast(FP8X4), rhs_scale=k_scales[:, cols],
-                    start=(g == 0), stop=(g == PASSES - 1),
+                    lhsT=q_codes[:, rows].bitcast(FP8X4),
+                    lhsT_scale=q_scales[:, rows],
+                    rhs=k_codes[:, cols].bitcast(FP8X4),
+                    rhs_scale=k_scales[:, cols],
+                    start=(g == 0),
+                    stop=(g == PASSES - 1),
                 )
 
         root = 1.0 / math.sqrt(HEAD)
@@ -328,80 +325,96 @@ def tile_ropeattention_pa_t_w4_kernel(
             nc.scalar.activation(out=res[:], in_=score_banks[grp, b][:], func=ACT.Copy, scale=root)
             nc.sync.dma_start(out=out[2 * grp + b].rearrange("(m p) n -> p m n", p=P), in_=res[:])
 
-        def due(slot, step):
-            res = []
-            for grp in range(1, GROUPS):
-                plan = PLAN_1 if grp == 1 else PLAN
-                base = 0 if grp == 1 else len(BLOCKS) * grp
-                when = plan[step]
-                for part, w in enumerate(when if isinstance(when, tuple) else (when,)):
-                    if max(base + w, 0) == slot:
-                        res.append((grp, part))
-            return res
-
-        def prepare_tensor(slot):
-            for grp, part in due(slot, "turn"):
-                turn(grp, 0)
-                turn(grp, 1)
-
-        def prepare_scalar(slot):
-            for grp, part in due(slot, "widen"):
-                if part == 0:
-                    new_wide(grp)
-                widen(nc.scalar.copy, grp, 2 * part, 2 * part + 2)
-            for grp, part in due(slot, "leave"):
-                if part == 0:
-                    new_split(grp)
-                leave_scalar(grp, part)
-            for grp, part in due(slot, "zip"):
-                if part == 0:
-                    new_zipped(grp)
-                zip_x(nc.scalar.copy, grp, S * part, S * (part + 1))
-            for grp, part in due(slot, "negate"):
-                if grp in NEG_SCALAR:
-                    negate(grp, "S")
-
-        def prepare_vector(slot):
-            for grp, part in due(slot, "negate"):
-                if grp not in NEG_SCALAR:
-                    negate(grp, "D")
-            for grp, part in due(slot, "plus"):
-                quantize_x(grp, 0)
-            for grp, part in due(slot, "minus"):
-                quantize_x(grp, 1)
-
         new_wide(0)
-        for n in range(FIRST_TILES):
-            widen(nc.vector.tensor_copy, 0, n, n + 1)
         for n in range(FIRST_TILES, TILES):
             widen(nc.scalar.copy, 0, n, n + 1)
+        nc.vector.tensor_tensor(out=factor3[:], in0=factor[:, 0:3], in1=factor[:, 3:6], op=ALU.mult)
+        widen(nc.vector.tensor_copy, 0, 0, 1)
+        nc.vector.tensor_tensor(out=factor2[:, 0:1], in0=factor3[:, 0:1], in1=factor[:, 6:7], op=ALU.mult)
+        nc.vector.tensor_tensor(out=factor2[:, 1:2], in0=factor3[:, 1:2], in1=factor3[:, 2:3], op=ALU.mult)
+        for n in range(1, FIRST_TILES):
+            widen(nc.vector.tensor_copy, 0, n, n + 1)
+        new_wide(1)
+        widen(nc.scalar.copy, 1, 0, 2)
         turn(0, 0)
         turn(0, 1)
-        finish_angles()
+        nc.vector.tensor_tensor(out=omega[:, 0:1], in0=factor2[:, 0:1], in1=factor2[:, 1:2], op=ALU.mult)
         sort_words(QUERY, 0)
+        nc.vector.tensor_scalar(out=angle[:], in0=position[:], scalar1=omega[:, 0:1], scalar2=None, op0=ALU.mult)
+        nc.vector.tensor_scalar(out=omega[:, 1:2], in0=omega[:, 0:1], scalar1=rho**P, scalar2=None, op0=ALU.mult)
+        make_bias(QUERY)
+        nc.vector.tensor_scalar(
+            out=turns[:], in0=angle[:], scalar1=1.0 / (2.0 * math.pi), scalar2=None, op0=ALU.mult
+        )
+        nc.vector.tensor_scalar(out=omega[:, 2:3], in0=omega[:, 0:1], scalar1=-(rho**P), scalar2=None, op0=ALU.mult)
         new_split(0)
         for t in (0, 1):
             leave_scalar(0, t)
-        for t in (2, 3):
-            leave_vector(0, t)
+        leave_vector(0, 2)
+        nc.vector.scalar_tensor_tensor(
+            out=reduced1[:], in0=turns[:], scalar=-coarse, in1=angle[:], op0=ALU.mult, op1=ALU.add
+        )
+        leave_vector(0, 3)
+        nc.vector.scalar_tensor_tensor(
+            out=reduced2[:], in0=turns[:], scalar=coarse - 2.0 * math.pi, in1=reduced1[:], op0=ALU.mult, op1=ALU.add
+        )
+        widen(nc.scalar.copy, 1, 2, 3)
         new_zipped(0)
+        zip_planes(nc.vector.tensor_copy, zipped[0], split[0], 0, FIRST_ZIP)
+        zip_planes(nc.scalar.copy, zipped[0], split[0], FIRST_ZIP, TOK)
+        table_0()
         sort_scales(QUERY, 0)
-        zip_x(nc.vector.tensor_copy, 0, 0, FIRST_VECTOR)
-        zip_x(nc.scalar.copy, 0, FIRST_VECTOR, TOK)
-        make_table(0)
         quantize_x(0, 0)
-        negate(0, "D")
-        make_bias(QUERY)
+        negate(0)
+        sort_words(QUERY, 1)
         quantize_x(0, 1)
-        new_wide(1)
-        widen(nc.scalar.copy, 1, 0, TILES)
-        make_table(1)
+        sort_scales(QUERY, 1)
+        widen(nc.scalar.copy, 1, 3, TILES)
+        table_1()
+
+        def due(blk, name):
+            res = []
+            for grp in range(1, GROUPS):
+                for part, when in enumerate((PLAN_1 if grp == 1 else PLAN)[name]):
+                    if max(len(BLOCKS) * grp + when, 0) == blk:
+                        res.append((grp, part))
+            return res
+
+        def prepare_tensor(blk):
+            for grp, part in due(blk, "turn"):
+                turn(grp, 0)
+                turn(grp, 1)
+
+        def prepare_scalar(blk):
+            for grp, part in due(blk, "widen"):
+                if part == 0:
+                    new_wide(grp)
+                widen(nc.scalar.copy, grp, 2 * part, 2 * part + 2)
+            for grp, part in due(blk, "leave"):
+                if part == 0:
+                    new_split(grp)
+                leave_scalar(grp, part)
+            for grp, part in due(blk, "zip"):
+                if part == 0:
+                    new_zipped(grp)
+                zip_planes(nc.scalar.copy, zipped[grp], split[grp], S * part, S * (part + 1))
+            for grp, part in due(blk, "negate"):
+                if grp in NEGATED_BY_SCALAR:
+                    negate(grp)
+
+        def prepare_vector(blk):
+            for grp, part in due(blk, "negate"):
+                if grp not in NEGATED_BY_SCALAR:
+                    negate(grp)
+            for grp, part in due(blk, "plus"):
+                quantize_x(grp, 0)
+            for grp, part in due(blk, "minus"):
+                quantize_x(grp, 1)
 
         for blk in range(LAST + 1):
             new_rotated(blk)
             if blk > 0:
-                mark_ready(blk - 1, ZIP_SCALAR)
-                zip_gpsimd(blk - 1, ZIP_SCALAR, TOK)
+                zip_gpsimd(blk - 1)
             for r in PLANES:
                 project(blk, r)
                 if blk < LAST:
@@ -414,36 +427,38 @@ def tile_ropeattention_pa_t_w4_kernel(
             prepare_scalar(blk)
             for grp in range(GROUPS):
                 for b in range(2):
-                    if blk == len(BLOCKS) * grp + SCORES + b:
+                    if blk == len(BLOCKS) * grp + SCORES_AFTER + b:
                         scores(grp, b)
                         store(grp, b)
             new_ready(blk)
             if blk < LAST:
-                zip_copy(nc.scalar.copy, blk, 0, ZIP_SCALAR)
-            if blk < 3:
-                sort_words(*BLOCKS[blk + 1])
-                sort_scales(*BLOCKS[blk + 1])
+                zip_planes(nc.scalar.copy, ready[blk], rotated[blk], 0, ZIP_SCALAR)
+            if blk < 2:
+                sort_words(*BLOCKS[blk + 2])
+                sort_scales(*BLOCKS[blk + 2])
             if blk == 1:
                 make_bias(KEY)
-            if blk >= LAG:
-                quantize_qk(blk - LAG, 0, TOK)
+            if blk >= QUANTIZE_AFTER:
+                quantize_qk(blk - QUANTIZE_AFTER, 0, TOK)
             prepare_vector(blk)
-        zip_copy(nc.scalar.copy, LAST, 0, S)
-        zip_copy(nc.vector.tensor_copy, LAST, S, S + TAIL_VECTOR)
-        zip_copy(nc.scalar.copy, LAST, S + TAIL_VECTOR, TOK)
-        for back in range(LAG - 1, 0, -1):
-            quantize_qk(LAST - back, 0, TOK)
+
+        scores(GROUPS - 2, 1)
+        store(GROUPS - 2, 1)
+        zip_planes(nc.scalar.copy, ready[LAST], rotated[LAST], 0, S)
+        zip_planes(nc.vector.tensor_copy, ready[LAST], rotated[LAST], S, S + TAIL_ZIP)
+        zip_planes(nc.scalar.copy, ready[LAST], rotated[LAST], S + TAIL_ZIP, TOK)
+        quantize_qk(LAST - 1, 0, TOK)
         quantize_qk(LAST, 0, S)
         scores(GROUPS - 1, 0)
         quantize_qk(LAST, S, TOK)
         ends = []
         for m in range(2):
-            bank = ps_aux.tile([P, S], F32, name="bank_end%d" % m, tag="aux")
-            score(GROUPS - 1, 1, m, bank[:])
-            ends.append(bank)
-        res = roll.tile([P, 2, S], F32, name="res_end")
+            bank_end = ps_aux.tile([P, S], F32, name="bank_end%d" % m, tag="aux")
+            score(GROUPS - 1, 1, m, bank_end[:])
+            ends.append(bank_end)
+        res_end = keep.tile([P, 2, S], F32)
         store(GROUPS - 1, 0)
-        nc.vector.tensor_scalar(out=res[:, 0, :], in0=ends[0][:], scalar1=root, scalar2=None, op0=ALU.mult)
-        nc.sync.dma_start(out=out[B - 1, 0:P, :], in_=res[:, 0, :])
-        nc.scalar.activation(out=res[:, 1, :], in_=ends[1][:], func=ACT.Copy, scale=root)
-        nc.sync.dma_start(out=out[B - 1, P:S, :], in_=res[:, 1, :])
+        nc.vector.tensor_scalar(out=res_end[:, 0, :], in0=ends[0][:], scalar1=root, scalar2=None, op0=ALU.mult)
+        nc.sync.dma_start(out=out[B - 1, 0:P, :], in_=res_end[:, 0, :])
+        nc.scalar.activation(out=res_end[:, 1, :], in_=ends[1][:], func=ACT.Copy, scale=root)
+        nc.sync.dma_start(out=out[B - 1, P:S, :], in_=res_end[:, 1, :])

import math
from contextlib import ExitStack

import concourse.mybir as mybir
from concourse.masks import make_identity

F32 = mybir.dt.float32
BF16 = mybir.dt.bfloat16
I32 = mybir.dt.int32
U32 = mybir.dt.uint32
U8 = mybir.dt.uint8
FP8 = mybir.dt.float8_e4m3fn
FP8X4 = mybir.dt.float8_e4m3fn_x4
FP4X4 = mybir.dt.float4_e2m1fn_x4
ALU = mybir.AluOpType
ACT = mybir.ActivationFunctionType

P = 128
PACK = 4
WORD4 = 2
B, S, D, H = 16, 256, 512, 1024
HEAD = H // 2
ANGLES = H // 4
TOK = 2 * S
GROUPS = B * S // TOK
TILES = TOK // P
PASSES = H // (P * PACK)
QUERY, KEY = 0, 1
BLOCKS = [(QUERY, 0), (QUERY, 1), (KEY, 0), (KEY, 1)]
LAST = len(BLOCKS) * GROUPS - 1
PLANES = (1, 3, 0, 2)
BITS = 7

ZIP_SCALAR = 240
FIRST_TILES = 2
FIRST_ZIP = 352
TAIL_ZIP = 160
NEGATED_BY_SCALAR = (2, 4, 6, 7)

PLAN = dict(widen=(-10, -9), turn=(-7,), leave=(-7, -6, -6, -5), zip=(-5, -4), negate=(-3,), plus=(-3,), minus=(-2,))
PLAN_1 = dict(widen=(), turn=(-4,), leave=(-4, -4, -4, -4), zip=(-3, -3), negate=(-2,), plus=(-2,), minus=(-2,))
QUANTIZE_AFTER = 2
SCORES_AFTER = 7

FLOPS = 2 * B * S * D * 2 * H + 2 * B * S * S * H


def tile_ropeattention_pa_t_w4_kernel(
    tc, hidden_bytes, hidden_scale, wq_words, wq_scales, bq, wk_words, wk_scales, bk, out
):
    nc = tc.nc
    with ExitStack() as ctx:
        keep = ctx.enter_context(tc.tile_pool(name="keep", bufs=1))
        work = ctx.enter_context(tc.tile_pool(name="work", bufs=3))
        roll = ctx.enter_context(tc.tile_pool(name="roll", bufs=5))
        ps_proj = ctx.enter_context(tc.psum_pool(name="ps_proj", bufs=5))
        ps_aux = ctx.enter_context(tc.psum_pool(name="ps_aux", bufs=3))
        ctx.enter_context(tc.manual_schedule())

        scale_col = keep.tile([P, PACK], F32)
        nc.scalar.dma_start(out=scale_col[:], in_=hidden_scale.rearrange("a b (p t) -> p (a b t)", t=PACK))

        tokens = hidden_bytes.rearrange("b s k -> (b s) k")
        x_bytes = keep.tile([P, GROUPS, TILES, D], U8, align_bytes=64)

        def load_x(grp, n0, n1):
            rows = tokens[grp * TOK : (grp + 1) * TOK, :].rearrange("(n p) k -> p n k", p=P)
            nc.sync.dma_start(out=x_bytes[:, grp, n0:n1, :], in_=rows[:, n0:n1, :])

        load_x(0, 0, 2)
        load_x(0, 2, TILES)
        load_x(1, 0, TILES)
        w_raw = keep.tile([P, 2, WORD4 * H], U8, align_bytes=64)
        s_raw = keep.tile([P, 2, H], U8, align_bytes=64)
        nc.sync.dma_start(out=w_raw[:, QUERY, :], in_=wq_words[0])

        one = keep.tile([P, 1], F32)
        nc.vector.memset(one[:], 1.0)
        warm = keep.tile([P, 1], F32)
        nc.scalar.activation(out=warm[:], in_=one[:], func=ACT.Sin)
        nc.vector.memset(s_raw[:].rearrange("p a n -> p (a n)").bitcast(I32), 0)
        part_no = keep.tile([P, BITS], I32)
        nc.gpsimd.iota(part_no[:], pattern=[[0, BITS]], base=0, channel_multiplier=1)
        position = keep.tile([P, S], F32)
        nc.gpsimd.iota(
            position[:], pattern=[[1, S]], base=0, channel_multiplier=0, allow_small_or_imprecise_dtypes=True
        )
        ident = keep.tile([P, P], F32)
        make_identity(nc, ident[:])

        b_raw = []

        def load_scales_and_bias(i, s, b):
            for q in range(4):
                nc.sync.dma_start(
                    out=s_raw[32 * q : 32 * q + 4, i, :].bitcast(I32), in_=s[0, 4 * q : 4 * q + 4, :].bitcast(I32)
                )
            br = keep.tile([P, PASSES, PACK], BF16, name="b_raw%d" % i)
            nc.sync.dma_start(out=br[:], in_=b.rearrange("(g p r) -> p g r", p=P, r=PACK))
            b_raw.append(br)

        load_scales_and_bias(QUERY, wq_scales, bq)
        nc.sync.dma_start(out=w_raw[:, KEY, :], in_=wk_words[0])
        load_scales_and_bias(KEY, wk_scales, bk)
        for grp in range(2, GROUPS):
            load_x(grp, 0, TILES)

        rho = 10000.0 ** (-1.0 / ANGLES)
        mask = keep.tile([P, BITS], I32)
        for b in range(BITS):
            nc.vector.memset(mask[:, b : b + 1], 1 << b)
        slope = keep.tile([P, BITS], F32)
        for b in range(BITS):
            nc.vector.tensor_scalar(
                out=slope[:, b : b + 1], in0=one[:], scalar1=(rho ** (1 << b) - 1.0) / (1 << b), scalar2=None,
                op0=ALU.mult,
            )
        half_pi = keep.tile([P, 1], F32)
        nc.vector.tensor_scalar(out=half_pi[:], in0=one[:], scalar1=math.pi / 2.0, scalar2=None, op0=ALU.mult)
        bits = keep.tile([P, BITS], I32)
        nc.vector.tensor_tensor(out=bits[:], in0=part_no[:], in1=mask[:], op=ALU.bitwise_and)
        step = keep.tile([P, BITS], F32)
        nc.vector.tensor_tensor(out=step[:], in0=bits[:], in1=slope[:], op=ALU.mult)
        factor = keep.tile([P, BITS], F32)
        nc.vector.tensor_scalar(out=factor[:], in0=step[:], scalar1=1.0, scalar2=None, op0=ALU.add)

        factor3 = keep.tile([P, 3], F32)
        factor2 = keep.tile([P, 2], F32)
        omega = keep.tile([P, 3], F32)
        angle = keep.tile([P, S], F32)
        turns = keep.tile([P, S], I32)
        reduced1 = keep.tile([P, S], F32)
        reduced2 = keep.tile([P, S], F32)
        reduced_abs = keep.tile([P, S], F32)
        table = keep.tile([P, 2 * PASSES, TOK], F32)
        coarse = 6.28125

        def table_0():
            nc.scalar.activation(out=reduced_abs[:], in_=reduced2[:], func=ACT.Abs)
            for b in range(TOK // S):
                cols = slice(b * S, (b + 1) * S)
                nc.scalar.activation(out=table[:, 0, cols], in_=reduced2[:], func=ACT.Sin)
                nc.scalar.activation(
                    out=table[:, 1, cols], in_=reduced_abs[:], func=ACT.Sin, bias=half_pi[:], scale=-1.0
                )

        def table_1():
            for b in range(TOK // S):
                cols = slice(b * S, (b + 1) * S)
                nc.scalar.activation(out=table[:, 2, cols], in_=position[:], func=ACT.Sin, scale=omega[:, 1:2])
                nc.scalar.activation(
                    out=table[:, 3, cols], in_=position[:], func=ACT.Sin, bias=half_pi[:], scale=omega[:, 2:3]
                )

        w_perm = keep.tile([P, 2, PASSES, PACK, WORD4 * P], U8, align_bytes=64)
        s_perm = keep.tile([P, 2, PASSES, PACK, P], U8, align_bytes=64)
        bias = keep.tile([P, 2, PASSES, PACK], F32)

        def sort_words(i, g):
            n = WORD4 * P * PACK
            nc.vector.tensor_copy(
                out=w_perm[:, i, g].rearrange("p r (c b) -> p r c b", b=WORD4),
                in_=w_raw[:, i, g * n : (g + 1) * n].rearrange("p (c r b) -> p r c b", r=PACK, b=WORD4),
            )

        def sort_scales(i, g):
            n = P * PACK
            nc.vector.tensor_copy(
                out=s_perm[:, i, g], in_=s_raw[:, i, g * n : (g + 1) * n].rearrange("p (c r) -> p r c", r=PACK)
            )

        def make_bias(i):
            raw = b_raw[i][:].rearrange("p g (h two) -> p (g h) two", two=2)
            res = bias[:, i].rearrange("p g (h two) -> p (g h) two", two=2)
            nc.vector.tensor_tensor(out=res[:, :, 0], in0=raw[:, :, 0], in1=raw[:, :, 1], op=ALU.subtract)
            nc.vector.tensor_tensor(out=res[:, :, 1], in0=raw[:, :, 0], in1=raw[:, :, 1], op=ALU.add)

        wide, turned, split, zipped, negated, x_codes = {}, {}, {}, {}, {}, {}

        def new_wide(grp):
            xw = work.tile([P, TILES, D], BF16, name="xw", align_bytes=64)
            wide[grp] = xw

        def widen(copy, grp, n0, n1):
            copy(
                out=wide[grp][:, n0:n1, :].rearrange("p n k -> p (n k)"),
                in_=x_bytes[:, grp, n0:n1, :].rearrange("p n k -> p (n k)").bitcast(FP8),
            )

        def turn(grp, u):
            bank = ps_aux.tile([P, TILES, P], F32, name="bank_turn", tag="aux")
            turned[grp, u] = bank
            for n in range(TILES):
                words = wide[grp][:, n, :].bitcast(F32)
                nc.tensor.transpose(bank[:, n, :], words[:, u : D // 2 : 2], ident[:])

        def new_split(grp):
            xs = work.tile([P, PACK, TOK], BF16, name="xs", align_bytes=64)
            split[grp] = xs

        def leave_operands(grp, t):
            u, e = divmod(t, 2)
            words = turned[grp, u][:].rearrange("p n c -> p (n c)")
            halves = words.bitcast(BF16).rearrange("p (c e) -> p c e", e=2)
            return split[grp][:, t, :], halves[:, :, e], scale_col[:, t : t + 1]

        def leave_scalar(grp, t):
            dst, src, scale = leave_operands(grp, t)
            nc.scalar.activation(out=dst, in_=src, func=ACT.Copy, scale=scale)

        def leave_vector(grp, t):
            dst, src, scale = leave_operands(grp, t)
            nc.vector.tensor_scalar(out=dst, in0=src, scalar1=scale, scalar2=None, op0=ALU.mult)

        def zip_planes(copy, dst, src, c0, c1):
            copy(
                out=dst[:, c0:c1, :].rearrange("p (c i) t -> p c t i", i=4),
                in_=src[:, :, c0:c1].rearrange("p t (c i) -> p c t i", i=4),
            )

        def new_zipped(grp):
            xz = work.tile([P, TOK, PACK], BF16, name="xz", align_bytes=64)
            zipped[grp] = xz

        def negate(grp):
            xn = work.tile([P, TOK, PACK], BF16, name="xn", align_bytes=64)
            negated[grp] = xn
            if grp in NEGATED_BY_SCALAR:
                nc.scalar.activation(out=xn[:], in_=zipped[grp][:], func=ACT.Copy, scale=-1.0)
            else:
                nc.vector.tensor_scalar(out=xn[:], in0=zipped[grp][:], scalar1=-1.0, scalar2=None, op0=ALU.mult)

        def quantize_x(grp, minus):
            codes = work.tile([P, TOK], U32, name="x_codes%d" % minus, align_bytes=64)
            scales = work.tile([P, TOK], U8, name="x_scales%d" % minus, align_bytes=64)
            x_codes[grp, minus] = (codes, scales)
            src = (negated if minus else zipped)[grp]
            nc.vector.quantize_mx(
                out=codes[:].bitcast(FP8X4), scales=scales[:], in_=src[:].rearrange("p c t -> p (c t)")
            )

        sums, rotated, ready, qk_codes, score_banks = {}, {}, {}, {}, {}

        def project(blk, r):
            grp, j = divmod(blk, len(BLOCKS))
            i, g = BLOCKS[j]
            acc = ps_proj.tile([P, TOK], F32, name="acc")
            sums[blk, r] = acc
            even = r // 2 * 2
            for odd in range(2):
                minus = 1 if odd == 1 and r % 2 == 0 else 0
                codes, scales = x_codes[grp, minus]
                nc.tensor.matmul_mx(
                    out=acc[:],
                    lhsT=w_perm[:, i, g, even + odd, :].bitcast(FP4X4),
                    lhsT_scale=s_perm[:, i, g, even + odd, :],
                    rhs=codes[:].bitcast(FP8X4),
                    rhs_scale=scales[:],
                    start=(odd == 0),
                    stop=(odd == 1),
                )

        def new_rotated(blk):
            rot = roll.tile([P, PACK, TOK], BF16, name="rot", align_bytes=64)
            rotated[blk] = rot

        def rotate(blk, r, c0, c1):
            i, g = BLOCKS[blk % len(BLOCKS)]
            nc.vector.scalar_tensor_tensor(
                out=rotated[blk][:, r, c0:c1], in0=sums[blk, r][:, c0:c1], scalar=bias[:, i, g, r : r + 1],
                in1=table[:, 2 * g + r // 2, c0:c1], op0=ALU.add, op1=ALU.mult,
            )

        def new_ready(blk):
            rdy = roll.tile([P, TOK, PACK], BF16, name="rdy", align_bytes=64)
            ready[blk] = rdy

        def zip_gpsimd(blk):
            nc.vector.memset(ready[blk][:, ZIP_SCALAR : ZIP_SCALAR + PACK, :], 0.0)
            nc.gpsimd.tensor_scalar(
                out=ready[blk][:, ZIP_SCALAR:TOK, :],
                in0=rotated[blk][:, :, ZIP_SCALAR:TOK].rearrange("p t c -> p c t"),
                scalar1=1.0, scalar2=1.0, op0=ALU.mult, op1=ALU.mult,
            )

        def quantize_qk(blk, c0, c1):
            if c0 == 0:
                j = blk % len(BLOCKS)
                new_codes = roll.tile([P, TOK], U32, name="codes%d" % j, align_bytes=64)
                new_scales = roll.tile([P, TOK], U8, name="scales%d" % j, align_bytes=64)
                qk_codes[blk] = (new_codes, new_scales)
            codes, scales = qk_codes[blk]
            nc.vector.quantize_mx(
                out=codes[:, c0:c1].bitcast(FP8X4),
                scales=scales[:, c0:c1],
                in_=ready[blk][:, c0:c1, :].rearrange("p c t -> p (c t)"),
            )

        def score(grp, b, m, bank):
            rows = slice(b * S + m * P, b * S + (m + 1) * P)
            cols = slice(b * S, (b + 1) * S)
            for g in range(PASSES):
                q_codes, q_scales = qk_codes[len(BLOCKS) * grp + g]
                k_codes, k_scales = qk_codes[len(BLOCKS) * grp + PASSES + g]
                nc.tensor.matmul_mx(
                    out=bank,
                    lhsT=q_codes[:, rows].bitcast(FP8X4),
                    lhsT_scale=q_scales[:, rows],
                    rhs=k_codes[:, cols].bitcast(FP8X4),
                    rhs_scale=k_scales[:, cols],
                    start=(g == 0),
                    stop=(g == PASSES - 1),
                )

        root = 1.0 / math.sqrt(HEAD)

        def scores(grp, b):
            bank = ps_aux.tile([P, 2, S], F32, name="bank_score", tag="aux")
            score_banks[grp, b] = bank
            for m in range(2):
                score(grp, b, m, bank[:, m, :])

        def store(grp, b):
            res = roll.tile([P, 2, S], F32, name="res")
            nc.scalar.activation(out=res[:], in_=score_banks[grp, b][:], func=ACT.Copy, scale=root)
            nc.sync.dma_start(out=out[2 * grp + b].rearrange("(m p) n -> p m n", p=P), in_=res[:])

        new_wide(0)
        for n in range(FIRST_TILES, TILES):
            widen(nc.scalar.copy, 0, n, n + 1)
        nc.vector.tensor_tensor(out=factor3[:], in0=factor[:, 0:3], in1=factor[:, 3:6], op=ALU.mult)
        widen(nc.vector.tensor_copy, 0, 0, 1)
        nc.vector.tensor_tensor(out=factor2[:, 0:1], in0=factor3[:, 0:1], in1=factor[:, 6:7], op=ALU.mult)
        nc.vector.tensor_tensor(out=factor2[:, 1:2], in0=factor3[:, 1:2], in1=factor3[:, 2:3], op=ALU.mult)
        for n in range(1, FIRST_TILES):
            widen(nc.vector.tensor_copy, 0, n, n + 1)
        new_wide(1)
        widen(nc.scalar.copy, 1, 0, 2)
        turn(0, 0)
        turn(0, 1)
        nc.vector.tensor_tensor(out=omega[:, 0:1], in0=factor2[:, 0:1], in1=factor2[:, 1:2], op=ALU.mult)
        sort_words(QUERY, 0)
        nc.vector.tensor_scalar(out=angle[:], in0=position[:], scalar1=omega[:, 0:1], scalar2=None, op0=ALU.mult)
        nc.vector.tensor_scalar(out=omega[:, 1:2], in0=omega[:, 0:1], scalar1=rho**P, scalar2=None, op0=ALU.mult)
        make_bias(QUERY)
        nc.vector.tensor_scalar(
            out=turns[:], in0=angle[:], scalar1=1.0 / (2.0 * math.pi), scalar2=None, op0=ALU.mult
        )
        nc.vector.tensor_scalar(out=omega[:, 2:3], in0=omega[:, 0:1], scalar1=-(rho**P), scalar2=None, op0=ALU.mult)
        new_split(0)
        for t in (0, 1):
            leave_scalar(0, t)
        leave_vector(0, 2)
        nc.vector.scalar_tensor_tensor(
            out=reduced1[:], in0=turns[:], scalar=-coarse, in1=angle[:], op0=ALU.mult, op1=ALU.add
        )
        leave_vector(0, 3)
        nc.vector.scalar_tensor_tensor(
            out=reduced2[:], in0=turns[:], scalar=coarse - 2.0 * math.pi, in1=reduced1[:], op0=ALU.mult, op1=ALU.add
        )
        widen(nc.scalar.copy, 1, 2, 3)
        new_zipped(0)
        zip_planes(nc.vector.tensor_copy, zipped[0], split[0], 0, FIRST_ZIP)
        zip_planes(nc.scalar.copy, zipped[0], split[0], FIRST_ZIP, TOK)
        table_0()
        sort_scales(QUERY, 0)
        quantize_x(0, 0)
        negate(0)
        sort_words(QUERY, 1)
        quantize_x(0, 1)
        sort_scales(QUERY, 1)
        widen(nc.scalar.copy, 1, 3, TILES)
        table_1()

        def due(blk, name):
            res = []
            for grp in range(1, GROUPS):
                for part, when in enumerate((PLAN_1 if grp == 1 else PLAN)[name]):
                    if max(len(BLOCKS) * grp + when, 0) == blk:
                        res.append((grp, part))
            return res

        def prepare_tensor(blk):
            for grp, part in due(blk, "turn"):
                turn(grp, 0)
                turn(grp, 1)

        def prepare_scalar(blk):
            for grp, part in due(blk, "widen"):
                if part == 0:
                    new_wide(grp)
                widen(nc.scalar.copy, grp, 2 * part, 2 * part + 2)
            for grp, part in due(blk, "leave"):
                if part == 0:
                    new_split(grp)
                leave_scalar(grp, part)
            for grp, part in due(blk, "zip"):
                if part == 0:
                    new_zipped(grp)
                zip_planes(nc.scalar.copy, zipped[grp], split[grp], S * part, S * (part + 1))
            for grp, part in due(blk, "negate"):
                if grp in NEGATED_BY_SCALAR:
                    negate(grp)

        def prepare_vector(blk):
            for grp, part in due(blk, "negate"):
                if grp not in NEGATED_BY_SCALAR:
                    negate(grp)
            for grp, part in due(blk, "plus"):
                quantize_x(grp, 0)
            for grp, part in due(blk, "minus"):
                quantize_x(grp, 1)

        for blk in range(LAST + 1):
            new_rotated(blk)
            if blk > 0:
                zip_gpsimd(blk - 1)
            for r in PLANES:
                project(blk, r)
                if blk < LAST:
                    rotate(blk, r, 0, TOK)
            if blk == LAST:
                for b in range(2):
                    for r in PLANES:
                        rotate(blk, r, b * S, (b + 1) * S)
            prepare_tensor(blk)
            prepare_scalar(blk)
            for grp in range(GROUPS):
                for b in range(2):
                    if blk == len(BLOCKS) * grp + SCORES_AFTER + b:
                        scores(grp, b)
                        store(grp, b)
            new_ready(blk)
            if blk < LAST:
                zip_planes(nc.scalar.copy, ready[blk], rotated[blk], 0, ZIP_SCALAR)
            if blk < 2:
                sort_words(*BLOCKS[blk + 2])
                sort_scales(*BLOCKS[blk + 2])
            if blk == 1:
                make_bias(KEY)
            if blk >= QUANTIZE_AFTER:
                quantize_qk(blk - QUANTIZE_AFTER, 0, TOK)
            prepare_vector(blk)

        scores(GROUPS - 2, 1)
        store(GROUPS - 2, 1)
        zip_planes(nc.scalar.copy, ready[LAST], rotated[LAST], 0, S)
        zip_planes(nc.vector.tensor_copy, ready[LAST], rotated[LAST], S, S + TAIL_ZIP)
        zip_planes(nc.scalar.copy, ready[LAST], rotated[LAST], S + TAIL_ZIP, TOK)
        quantize_qk(LAST - 1, 0, TOK)
        quantize_qk(LAST, 0, S)
        scores(GROUPS - 1, 0)
        quantize_qk(LAST, S, TOK)
        ends = []
        for m in range(2):
            bank_end = ps_aux.tile([P, S], F32, name="bank_end%d" % m, tag="aux")
            score(GROUPS - 1, 1, m, bank_end[:])
            ends.append(bank_end)
        res_end = keep.tile([P, 2, S], F32)
        store(GROUPS - 1, 0)
        nc.vector.tensor_scalar(out=res_end[:, 0, :], in0=ends[0][:], scalar1=root, scalar2=None, op0=ALU.mult)
        nc.sync.dma_start(out=out[B - 1, 0:P, :], in_=res_end[:, 0, :])
        nc.scalar.activation(out=res_end[:, 1, :], in_=ends[1][:], func=ACT.Copy, scale=root)
        nc.sync.dma_start(out=out[B - 1, P:S, :], in_=res_end[:, 1, :])
